import numpy as np
import ml_dtypes


def mxq(x, axis, fmt="e4m3"):
    dtype, down = {"e4m3": (ml_dtypes.float8_e4m3fn, 7), "e5m2": (ml_dtypes.float8_e5m2, 14)}[fmt]
    v = np.moveaxis(np.asarray(x, np.float32).astype(ml_dtypes.bfloat16).astype(np.float64), axis, -1)
    blocks = v.reshape(v.shape[:-1] + (-1, 32))
    amax = np.abs(blocks).max(-1, keepdims=True)
    byte = np.maximum(np.where(amax > 0, np.frexp(amax)[1] - 1 + 127, 0) - down, 1)
    scale = np.exp2(byte - 127.0)
    codes = (blocks / scale).astype(np.float32).astype(dtype).astype(np.float64)
    return np.moveaxis((codes * scale).reshape(v.shape), -1, axis)


WIDE = False


def mx_kscale(k):
    if not WIDE:
        return np.ones(k)
    levels = np.array([10, -10, 5, -5, 0])
    a = np.random.permutation(np.resize(levels, k // 512 * 4)).reshape(k // 512, 4)
    idx = np.arange(k)
    return np.exp2(a[idx // 512, idx % 128 // 32])


BF16 = ml_dtypes.bfloat16


def bf(x):
    return np.asarray(x, np.float32).astype(BF16)


def f64(x):
    return np.asarray(x).astype(np.float64)


E2M1 = np.array([0.0, 0.5, 1.0, 1.5, 2.0, 3.0, 4.0, 6.0, -0.0, -0.5, -1.0, -1.5, -2.0, -3.0, -4.0, -6.0])


def pack_weight(w, fmt):
    k, n = w.shape
    w = f64(bf(w)).reshape(k // 32, 32, n)
    amax = np.abs(w).max(1)
    if fmt == "e4m3":
        byte = np.frexp(amax)[1] - 1 + 127 - 7
    else:
        mant, ex = np.frexp(amax / 6.0)
        byte = np.where(mant > 0.5, ex, ex - 1) + 127
    byte = np.clip(np.where(amax > 0, byte, 1), 1, 254)
    scaled = (w * np.exp2(127.0 - byte)[:, None, :]).reshape(k, n).astype(np.float32)
    by_word = np.ascontiguousarray(scaled.reshape(k // 512, 128, 4, n).transpose(0, 1, 3, 2))
    if fmt == "e4m3":
        words = by_word.astype(ml_dtypes.float8_e4m3fn).view(np.uint8)
    else:
        c = by_word.astype(ml_dtypes.float4_e2m1fn).view(np.uint8) & 0xF
        words = c[..., 0::2] | (c[..., 1::2] << 4)
    return np.ascontiguousarray(words), np.ascontiguousarray(byte.astype(np.uint8).reshape(k // 512, 16, n))


def unpack_weight(words, scales, fmt):
    g, p, n, _ = words.shape
    if fmt == "e4m3":
        vals = np.ascontiguousarray(words).view(ml_dtypes.float8_e4m3fn).astype(np.float64)
    else:
        nib = np.empty((g, p, n, 4), np.uint8)
        nib[..., 0::2] = words & 0xF
        nib[..., 1::2] = words >> 4
        vals = E2M1[nib]
    vals = vals * np.repeat(np.exp2(scales.astype(np.float64) - 127.0), 8, axis=1)[..., None]
    return vals.transpose(0, 1, 3, 2).reshape(g * 512, n)

def pack4(w):
    words, scales = pack_weight(w, "e2m1")
    return words.reshape(words.shape[0], 128, -1), scales


def unpack4(words, scales):
    return unpack_weight(words.reshape(words.shape[0], 128, -1, 2), scales, "e2m1")


B, H, P, D, NF, DO, G = 2, 12, 32, 512, 8, 512, 5
N = D * H * P


def setup_inputs():
    s = mx_kscale(D)
    x = bf(np.random.standard_normal((B, H, P, D)) * s)
    lin_w = np.random.standard_normal((G * D, D)) * 0.3 / np.sqrt(D) / s
    words, scales = pack4(lin_w.T)
    return {
        "x": x,
        "lin_w_words": words,
        "lin_w_scales": scales,
        "lin_b": bf(np.random.standard_normal(G * D) * 0.1),
        "grid": bf(np.arange(NF)[None, :] + 1.0 + 0.1 * np.random.standard_normal((G, NF))),
        "coef": bf(np.random.standard_normal((N, NF, G)) * 0.5),
        "shift": bf(np.random.standard_normal((1, H, G, P, D)) * 0.5),
    }


def reference(x, lin_w_words, lin_w_scales, lin_b, grid, coef, shift):
    xl = (mxq(f64(x), 3, "e4m3") @ unpack4(lin_w_words, lin_w_scales)) + f64(lin_b)
    xl = xl.reshape(B, G, N)
    sn = np.sin(f64(grid)[None, :, :, None] * xl[:, :, None, :])
    f = sn * f64(coef).transpose(2, 1, 0)[None]
    return f.reshape(B, H, G, NF, P, D).sum(axis=3) + f64(shift)

@@ -1,0 +1,205 @@
+import math
+from contextlib import ExitStack
+
+import concourse.mybir as mybir
+from concourse.masks import make_identity
+
+F32 = mybir.dt.float32
+BF16 = mybir.dt.bfloat16
+I32 = mybir.dt.int32
+U8 = mybir.dt.uint8
+U32 = mybir.dt.uint32
+FP8X4 = mybir.dt.float8_e4m3fn_x4
+FP4X4 = mybir.dt.float4_e2m1fn_x4
+ALU = mybir.AluOpType
+ACT = mybir.ActivationFunctionType
+
+P = 128
+B, H, POS, D, NF, G = 2, 12, 32, 512, 8, 5
+ROWS = B * H * POS
+ROWS_B = H * POS
+ROW_TILES = ROWS // P
+COLS = G * D
+COL_BLOCKS = COLS // P
+BLOCKS_B = ROWS_B * COL_BLOCKS
+CHUNKS = 12
+QUAD = 4
+QUADS_J = NF * CHUNKS // QUAD
+OUT_J = QUADS_J // 2
+PLANES = NF * G
+WORDS = PLANES // 2
+TWO_PI = 2.0 * math.pi
+
+FLOPS = 2 * ROWS * D * COLS
+
+
+def tile_ka_attention_heads_mod_pa_kernel(
+    tc, x, lin_w_words, lin_w_scales, lin_b, grid, coef, shift, out
+):
+    nc = tc.nc
+    coef_v = coef.rearrange("(c q i) m j -> q c (i m j)", c=CHUNKS, q=P)
+    shift_v = shift.rearrange("o h g p (q i) -> (p q) (o h g) i", i=P)
+    out_v = out.rearrange("b h g p (q i) -> (p q) b (h g) i", i=P)
+
+    with ExitStack() as whole:
+        keep = whole.enter_context(tc.tile_pool(name="keep", bufs=1))
+        ident = keep.tile([P, P], F32)
+        make_identity(nc, ident[:])
+        xl = keep.tile([P, B, BLOCKS_B], F32)
+        coef_sb = keep.tile([P, CHUNKS, P * PLANES], BF16)
+        turns = keep.tile([P, PLANES], F32)
+        bias_t = keep.tile([P, COL_BLOCKS], F32)
+
+        with ExitStack() as first:
+            stage = first.enter_context(tc.tile_pool(name="stage", bufs=1))
+            ps_x = first.enter_context(tc.psum_pool(name="ps_x", bufs=2))
+            ps_b = first.enter_context(tc.psum_pool(name="ps_b", bufs=1))
+            ps_mm = first.enter_context(tc.psum_pool(name="ps_mm", bufs=3))
+
+            x_sb = stage.tile([P, ROW_TILES, D], BF16)
+            w_words = stage.tile([P, 2 * COLS], U8, align_bytes=64)
+            w_scales = stage.tile([P, COLS], U8, align_bytes=64)
+            b_rows = stage.tile([P, P], BF16)
+            g_raw = stage.tile([P, PLANES], BF16)
+            ident_bf = stage.tile([P, P], BF16)
+            grouped = stage.tile([P, ROWS * 4], BF16, align_bytes=64)
+            x_codes = stage.tile([P, ROWS], U32, align_bytes=64)
+            x_scales = stage.tile([P, ROWS], U8, align_bytes=64)
+
+            nc.vector.memset(w_scales[:].bitcast(I32), 0)
+            nc.vector.memset(b_rows[:], 0.0)
+            make_identity(nc, ident_bf[:])
+
+            nc.sync.dma_start(
+                out=x_sb[:],
+                in_=x.rearrange("b h p d -> (b h p) d").rearrange("(t r) d -> r t d", r=P),
+            )
+            for quadrant in range(4):
+                nc.sync.dma_start(
+                    out=w_scales[32 * quadrant : 32 * quadrant + 4, :].bitcast(I32),
+                    in_=lin_w_scales[0, 4 * quadrant : 4 * quadrant + 4, :].bitcast(I32),
+                )
+            nc.sync.dma_start(out=w_words[:].bitcast(I32), in_=lin_w_words[0].bitcast(I32))
+            nc.sync.dma_start(
+                out=b_rows[0:COL_BLOCKS, :], in_=lin_b.rearrange("(c i) -> c i", i=P)
+            )
+            nc.sync.dma_start(
+                out=g_raw[:], in_=grid.rearrange("j m -> (j m)").partition_broadcast(P)
+            )
+            for c in range(CHUNKS):
+                nc.sync.dma_start(out=coef_sb[:, c, :], in_=coef_v[:, c, :])
+
+            nc.vector.tensor_scalar(
+                out=turns[:], in0=g_raw[:], scalar1=1.0 / TWO_PI, scalar2=None, op0=ALU.mult
+            )
+            bt = ps_b.tile([P, P], BF16)
+            nc.tensor.transpose(bt[:], b_rows[:], ident_bf[:])
+            nc.vector.tensor_copy(out=bias_t[:], in_=bt[:, 0:COL_BLOCKS])
+
+            grouped_w = grouped[:].bitcast(F32).rearrange("p (r u) -> p r u", u=2)
+            for rt in range(ROW_TILES):
+                rows = slice(rt * P, (rt + 1) * P)
+                xt = ps_x.tile([P, 2, P], F32)
+                x_words = x_sb[:, rt, :].bitcast(F32)
+                for u in range(2):
+                    nc.tensor.transpose(xt[:, u, :], x_words[:, u : D // 2 : 2], ident[:])
+                nc.vector.tensor_copy(
+                    out=grouped_w[:, rows, :], in_=xt[:].rearrange("p u r -> p r u")
+                )
+            for rt in range(ROW_TILES):
+                rows = slice(rt * P, (rt + 1) * P)
+                nc.vector.quantize_mx(
+                    out=x_codes[:, rows].bitcast(FP8X4),
+                    scales=x_scales[:, rows],
+                    in_=grouped[:, rt * 4 * P : (rt + 1) * 4 * P],
+                )
+
+            for rt in range(ROW_TILES):
+                rows = slice(rt * P, (rt + 1) * P)
+                b, third = divmod(rt, ROW_TILES // B)
+                xl_rows = xl[:, b, :].rearrange("p (r c) -> p r c", c=COL_BLOCKS)
+                for a in range(COL_BLOCKS // 4):
+                    mm = ps_mm.tile([P, 4, P], F32)
+                    for g in range(4):
+                        cb = 4 * a + g
+                        nc.tensor.matmul_mx(
+                            out=mm[:, g, :],
+                            lhsT=w_words[:, cb * 2 * P : (cb + 1) * 2 * P].bitcast(FP4X4),
+                            lhsT_scale=w_scales[:, cb * P : (cb + 1) * P],
+                            rhs=x_codes[:, rows].bitcast(FP8X4),
+                            rhs_scale=x_scales[:, rows],
+                            start=True,
+                            stop=True,
+                        )
+                    nc.vector.tensor_tensor(
+                        out=xl_rows[:, third * P : (third + 1) * P, 4 * a : 4 * a + 4],
+                        in0=mm[:].rearrange("p g r -> p r g"),
+                        in1=bias_t[:, 4 * a : 4 * a + 4].unsqueeze(1).to_broadcast([P, P, 4]),
+                        op=ALU.add,
+                    )
+
+        periods = whole.enter_context(tc.tile_pool(name="periods", bufs=2))
+        waves = whole.enter_context(tc.tile_pool(name="waves", bufs=6))
+        shifts = whole.enter_context(tc.tile_pool(name="shifts", bufs=2))
+        results = whole.enter_context(tc.tile_pool(name="results", bufs=3))
+        ps_coef = whole.enter_context(tc.psum_pool(name="ps_coef", bufs=3))
+        ps_sum = whole.enter_context(tc.psum_pool(name="ps_sum", bufs=2))
+
+        for j in range(G):
+            shift_j = shifts.tile([P, OUT_J, P], BF16)
+            nc.sync.dma_start(out=shift_j[:], in_=shift_v[:, j * OUT_J : (j + 1) * OUT_J, :])
+            pair = []
+            for quad in range(QUADS_J):
+                m, cq = divmod(quad, CHUNKS // QUAD)
+                plane = m * G + j
+                turn = turns[:, j * NF + m : j * NF + m + 1]
+                y0 = (j * CHUNKS + cq * QUAD) * P
+                xq = xl[:, :, y0 : y0 + QUAD * P]
+
+                coef_t = ps_coef.tile([P, QUAD, P], F32)
+                for cl in range(QUAD):
+                    words = coef_sb[:, cq * QUAD + cl, :].bitcast(F32)
+                    nc.tensor.transpose(
+                        coef_t[:, cl, :], words[:, plane // 2 : P * WORDS : WORDS], ident[:]
+                    )
+
+                k = periods.tile([P, B, QUAD * P], I32)
+                nc.vector.tensor_scalar(out=k[:], in0=xq, scalar1=turn, scalar2=None, op0=ALU.mult)
+                wave = waves.tile([P, B, QUAD * P], F32)
+                nc.vector.scalar_tensor_tensor(
+                    out=wave[:], in0=xq, scalar=turn, in1=k[:], op0=ALU.mult, op1=ALU.subtract
+                )
+                nc.scalar.activation(out=wave[:], in_=wave[:], func=ACT.Sin, scale=TWO_PI)
+                halves = coef_t[:].bitcast(BF16).rearrange("p c (q h) -> p c q h", h=2)
+                wave4 = wave[:].rearrange("p b (c q) -> p b c q", c=QUAD)
+                nc.vector.tensor_tensor(
+                    out=wave4,
+                    in0=wave4,
+                    in1=halves[:, :, :, plane % 2].unsqueeze(1).to_broadcast([P, B, QUAD, P]),
+                    op=ALU.mult,
+                )
+                pair.append(wave)
+                if len(pair) < 2:
+                    continue
+
+                total = ps_sum.tile([P, B, P], F32)
+                for b in range(B):
+                    for t in range(2 * QUAD):
+                        nc.tensor.matmul(
+                            out=total[:, b, :],
+                            lhsT=pair[t // QUAD][:, b, (t % QUAD) * P : (t % QUAD + 1) * P],
+                            rhs=ident[:],
+                            start=(t == 0),
+                            stop=(t == 2 * QUAD - 1),
+                            is_transpose=True,
+                        )
+                pair = []
+                o = quad // 2
+                res = results.tile([P, B, P], F32)
+                nc.vector.tensor_tensor(
+                    out=res[:],
+                    in0=total[:],
+                    in1=shift_j[:, o, :].unsqueeze(1).to_broadcast([P, B, P]),
+                    op=ALU.add,
+                )
+                nc.sync.dma_start(out=out_v[:, :, j * OUT_J + o, :], in_=res[:])

@@ -138,7 +138,7 @@ def tile_ka_attention_heads_mod_pa_kernel(
                         op=ALU.add,
                     )
 
-        periods = whole.enter_context(tc.tile_pool(name="periods", bufs=2))
+        periods = whole.enter_context(tc.tile_pool(name="periods", bufs=3))
         waves = whole.enter_context(tc.tile_pool(name="waves", bufs=6))
         shifts = whole.enter_context(tc.tile_pool(name="shifts", bufs=2))
         results = whole.enter_context(tc.tile_pool(name="results", bufs=3))
@@ -164,7 +164,9 @@ def tile_ka_attention_heads_mod_pa_kernel(
                     )
 
                 k = periods.tile([P, B, QUAD * P], I32)
-                nc.vector.tensor_scalar(out=k[:], in0=xq, scalar1=turn, scalar2=None, op0=ALU.mult)
+                nc.gpsimd.tensor_scalar(
+                    out=k[:], in0=xq, scalar1=turn, scalar2=0.0, op0=ALU.mult, op1=ALU.add
+                )
                 wave = waves.tile([P, B, QUAD * P], F32)
                 nc.vector.scalar_tensor_tensor(
                     out=wave[:], in0=xq, scalar=turn, in1=k[:], op0=ALU.mult, op1=ALU.subtract

@@ -145,63 +145,101 @@ def tile_ka_attention_heads_mod_pa_kernel(
         ps_coef = whole.enter_context(tc.psum_pool(name="ps_coef", bufs=3))
         ps_sum = whole.enter_context(tc.psum_pool(name="ps_sum", bufs=2))
 
-        for j in range(G):
-            shift_j = shifts.tile([P, OUT_J, P], BF16)
-            nc.sync.dma_start(out=shift_j[:], in_=shift_v[:, j * OUT_J : (j + 1) * OUT_J, :])
-            pair = []
-            for quad in range(QUADS_J):
-                m, cq = divmod(quad, CHUNKS // QUAD)
-                plane = m * G + j
-                turn = turns[:, j * NF + m : j * NF + m + 1]
-                y0 = (j * CHUNKS + cq * QUAD) * P
-                xq = xl[:, :, y0 : y0 + QUAD * P]
+        n_units = OUT_J * G * 2
+        k_of, coef_of, wave_of, total_of, shift_of = {}, {}, {}, {}, {}
 
-                coef_t = ps_coef.tile([P, QUAD, P], F32)
-                for cl in range(QUAD):
-                    words = coef_sb[:, cq * QUAD + cl, :].bitcast(F32)
-                    nc.tensor.transpose(
-                        coef_t[:, cl, :], words[:, plane // 2 : P * WORDS : WORDS], ident[:]
+        def where(u):
+            o, rest = divmod(u, 2 * G)
+            j, half = divmod(rest, 2)
+            m, cq = divmod(2 * o + half, CHUNKS // QUAD)
+            return o, j, m, cq
+
+        def x_and_turn(u):
+            o, j, m, cq = where(u)
+            y0 = (j * CHUNKS + cq * QUAD) * P
+            return xl[:, :, y0 : y0 + QUAD * P], turns[:, j * NF + m : j * NF + m + 1]
+
+        def count_periods(u):
+            xq, turn = x_and_turn(u)
+            k = periods.tile([P, B, QUAD * P], I32)
+            nc.gpsimd.tensor_scalar(
+                out=k[:], in0=xq, scalar1=turn, scalar2=0.0, op0=ALU.mult, op1=ALU.add
+            )
+            k_of[u] = k
+
+        def turn_coef(u):
+            o, j, m, cq = where(u)
+            word = (m * G + j) // 2
+            coef_t = ps_coef.tile([P, QUAD, P], F32)
+            for cl in range(QUAD):
+                words = coef_sb[:, cq * QUAD + cl, :].bitcast(F32)
+                nc.tensor.transpose(coef_t[:, cl, :], words[:, word : P * WORDS : WORDS], ident[:])
+            coef_of[u] = coef_t
+
+        def sine(u):
+            xq, turn = x_and_turn(u)
+            wave = waves.tile([P, B, QUAD * P], F32)
+            nc.vector.scalar_tensor_tensor(
+                out=wave[:], in0=xq, scalar=turn, in1=k_of.pop(u)[:], op0=ALU.mult, op1=ALU.subtract
+            )
+            nc.scalar.activation(out=wave[:], in_=wave[:], func=ACT.Sin, scale=TWO_PI)
+            wave_of[u] = wave
+
+        def weigh(u):
+            o, j, m, cq = where(u)
+            halves = coef_of.pop(u)[:].bitcast(BF16).rearrange("p c (q h) -> p c q h", h=2)
+            wave4 = wave_of[u][:].rearrange("p b (c q) -> p b c q", c=QUAD)
+            nc.vector.tensor_tensor(
+                out=wave4,
+                in0=wave4,
+                in1=halves[:, :, :, (m * G + j) % 2].unsqueeze(1).to_broadcast([P, B, QUAD, P]),
+                op=ALU.mult,
+            )
+
+        def add_up(v):
+            pair = [wave_of.pop(2 * v), wave_of.pop(2 * v + 1)]
+            total = ps_sum.tile([P, B, P], F32)
+            for b in range(B):
+                for t in range(2 * QUAD):
+                    nc.tensor.matmul(
+                        out=total[:, b, :],
+                        lhsT=pair[t // QUAD][:, b, (t % QUAD) * P : (t % QUAD + 1) * P],
+                        rhs=ident[:],
+                        start=(t == 0),
+                        stop=(t == 2 * QUAD - 1),
+                        is_transpose=True,
                     )
+            total_of[v] = total
 
-                k = periods.tile([P, B, QUAD * P], I32)
-                nc.gpsimd.tensor_scalar(
-                    out=k[:], in0=xq, scalar1=turn, scalar2=0.0, op0=ALU.mult, op1=ALU.add
-                )
-                wave = waves.tile([P, B, QUAD * P], F32)
-                nc.vector.scalar_tensor_tensor(
-                    out=wave[:], in0=xq, scalar=turn, in1=k[:], op0=ALU.mult, op1=ALU.subtract
-                )
-                nc.scalar.activation(out=wave[:], in_=wave[:], func=ACT.Sin, scale=TWO_PI)
-                halves = coef_t[:].bitcast(BF16).rearrange("p c (q h) -> p c q h", h=2)
-                wave4 = wave[:].rearrange("p b (c q) -> p b c q", c=QUAD)
-                nc.vector.tensor_tensor(
-                    out=wave4,
-                    in0=wave4,
-                    in1=halves[:, :, :, plane % 2].unsqueeze(1).to_broadcast([P, B, QUAD, P]),
-                    op=ALU.mult,
-                )
-                pair.append(wave)
-                if len(pair) < 2:
-                    continue
+        def finish(v):
+            o, j = divmod(v, G)
+            if j == 0:
+                shift_o = shifts.tile([P, G, P], BF16)
+                nc.sync.dma_start(out=shift_o[:], in_=shift_v[:, o : G * OUT_J : OUT_J, :])
+                shift_of[o] = shift_o
+            res = results.tile([P, B, P], F32)
+            nc.vector.tensor_tensor(
+                out=res[:],
+                in0=total_of.pop(v)[:],
+                in1=shift_of[o][:, j, :].unsqueeze(1).to_broadcast([P, B, P]),
+                op=ALU.add,
+            )
+            nc.sync.dma_start(out=out_v[:, :, j * OUT_J + o, :], in_=res[:])
 
-                total = ps_sum.tile([P, B, P], F32)
-                for b in range(B):
-                    for t in range(2 * QUAD):
-                        nc.tensor.matmul(
-                            out=total[:, b, :],
-                            lhsT=pair[t // QUAD][:, b, (t % QUAD) * P : (t % QUAD + 1) * P],
-                            rhs=ident[:],
-                            start=(t == 0),
-                            stop=(t == 2 * QUAD - 1),
-                            is_transpose=True,
-                        )
-                pair = []
-                o = quad // 2
-                res = results.tile([P, B, P], F32)
-                nc.vector.tensor_tensor(
-                    out=res[:],
-                    in0=total[:],
-                    in1=shift_j[:, o, :].unsqueeze(1).to_broadcast([P, B, P]),
-                    op=ALU.add,
-                )
-                nc.sync.dma_start(out=out_v[:, :, j * OUT_J + o, :], in_=res[:])
+        with tc.manual_schedule():
+            for u in range(2):
+                count_periods(u)
+                turn_coef(u)
+            sine(0)
+            for u in range(n_units):
+                if u + 2 < n_units:
+                    count_periods(u + 2)
+                    turn_coef(u + 2)
+                if u + 1 < n_units:
+                    sine(u + 1)
+                weigh(u)
+                if u % 2 == 1:
+                    add_up(u // 2)
+                    if u >= 3:
+                        finish(u // 2 - 1)
+            finish(n_units // 2 - 1)

@@ -138,72 +138,94 @@ def tile_ka_attention_heads_mod_pa_kernel(
                         op=ALU.add,
                     )
 
-        periods = whole.enter_context(tc.tile_pool(name="periods", bufs=3))
-        waves = whole.enter_context(tc.tile_pool(name="waves", bufs=6))
+        periods = whole.enter_context(tc.tile_pool(name="periods", bufs=2))
+        waves = whole.enter_context(tc.tile_pool(name="waves", bufs=3))
         shifts = whole.enter_context(tc.tile_pool(name="shifts", bufs=2))
         results = whole.enter_context(tc.tile_pool(name="results", bufs=3))
-        ps_coef = whole.enter_context(tc.psum_pool(name="ps_coef", bufs=3))
+        ps_coef = whole.enter_context(tc.psum_pool(name="ps_coef", bufs=4))
         ps_sum = whole.enter_context(tc.psum_pool(name="ps_sum", bufs=2))
 
-        n_units = OUT_J * G * 2
+        n_planes = OUT_J * G
         k_of, coef_of, wave_of, total_of, shift_of = {}, {}, {}, {}, {}
 
-        def where(u):
-            o, rest = divmod(u, 2 * G)
-            j, half = divmod(rest, 2)
-            m, cq = divmod(2 * o + half, CHUNKS // QUAD)
-            return o, j, m, cq
+        def quads(v):
+            o, j = divmod(v, G)
+            return [divmod(2 * o + half, CHUNKS // QUAD) for half in range(2)]
 
-        def x_and_turn(u):
-            o, j, m, cq = where(u)
-            y0 = (j * CHUNKS + cq * QUAD) * P
-            return xl[:, :, y0 : y0 + QUAD * P], turns[:, j * NF + m : j * NF + m + 1]
+        def runs(v):
+            j = v % G
+            (m0, cq0), (m1, cq1) = quads(v)
+            pieces = [(m0, cq0, 0, 2)] if m0 == m1 else [(m0, cq0, 0, 1), (m1, cq1, 1, 1)]
+            found = []
+            for m, cq, first, n in pieces:
+                y0 = (j * CHUNKS + cq * QUAD) * P
+                found.append(
+                    (
+                        slice(first * QUAD * P, (first + n) * QUAD * P),
+                        xl[:, :, y0 : y0 + n * QUAD * P],
+                        turns[:, j * NF + m : j * NF + m + 1],
+                    )
+                )
+            return found
 
-        def count_periods(u):
-            xq, turn = x_and_turn(u)
-            k = periods.tile([P, B, QUAD * P], I32)
-            nc.gpsimd.tensor_scalar(
-                out=k[:], in0=xq, scalar1=turn, scalar2=0.0, op0=ALU.mult, op1=ALU.add
-            )
-            k_of[u] = k
+        def count_periods(v):
+            k = periods.tile([P, B, 2 * QUAD * P], I32)
+            for cols, xq, turn in runs(v):
+                nc.gpsimd.tensor_scalar(
+                    out=k[:, :, cols], in0=xq, scalar1=turn, scalar2=0.0, op0=ALU.mult, op1=ALU.add
+                )
+            k_of[v] = k
 
-        def turn_coef(u):
-            o, j, m, cq = where(u)
-            word = (m * G + j) // 2
-            coef_t = ps_coef.tile([P, QUAD, P], F32)
-            for cl in range(QUAD):
-                words = coef_sb[:, cq * QUAD + cl, :].bitcast(F32)
-                nc.tensor.transpose(coef_t[:, cl, :], words[:, word : P * WORDS : WORDS], ident[:])
-            coef_of[u] = coef_t
+        def turn_coef(v):
+            j = v % G
+            coef_of[v] = []
+            for m, cq in quads(v):
+                word = (m * G + j) // 2
+                coef_t = ps_coef.tile([P, QUAD, P], F32)
+                for cl in range(QUAD):
+                    words = coef_sb[:, cq * QUAD + cl, :].bitcast(F32)
+                    nc.tensor.transpose(
+                        coef_t[:, cl, :], words[:, word : P * WORDS : WORDS], ident[:]
+                    )
+                coef_of[v].append(coef_t)
 
-        def sine(u):
-            xq, turn = x_and_turn(u)
-            wave = waves.tile([P, B, QUAD * P], F32)
-            nc.vector.scalar_tensor_tensor(
-                out=wave[:], in0=xq, scalar=turn, in1=k_of.pop(u)[:], op0=ALU.mult, op1=ALU.subtract
-            )
+        def sine(v):
+            k = k_of.pop(v)
+            wave = waves.tile([P, B, 2 * QUAD * P], F32)
+            for cols, xq, turn in runs(v):
+                nc.vector.scalar_tensor_tensor(
+                    out=wave[:, :, cols],
+                    in0=xq,
+                    scalar=turn,
+                    in1=k[:, :, cols],
+                    op0=ALU.mult,
+                    op1=ALU.subtract,
+                )
             nc.scalar.activation(out=wave[:], in_=wave[:], func=ACT.Sin, scale=TWO_PI)
-            wave_of[u] = wave
+            wave_of[v] = wave
 
-        def weigh(u):
-            o, j, m, cq = where(u)
-            halves = coef_of.pop(u)[:].bitcast(BF16).rearrange("p c (q h) -> p c q h", h=2)
-            wave4 = wave_of[u][:].rearrange("p b (c q) -> p b c q", c=QUAD)
-            nc.vector.tensor_tensor(
-                out=wave4,
-                in0=wave4,
-                in1=halves[:, :, :, (m * G + j) % 2].unsqueeze(1).to_broadcast([P, B, QUAD, P]),
-                op=ALU.mult,
-            )
+        def weigh(v):
+            j = v % G
+            for half, (m, cq) in enumerate(quads(v)):
+                pairs = coef_of[v][half][:].bitcast(BF16).rearrange("p c (q h) -> p c q h", h=2)
+                part = wave_of[v][:, :, half * QUAD * P : (half + 1) * QUAD * P]
+                part = part.rearrange("p b (c q) -> p b c q", c=QUAD)
+                nc.vector.tensor_tensor(
+                    out=part,
+                    in0=part,
+                    in1=pairs[:, :, :, (m * G + j) % 2].unsqueeze(1).to_broadcast([P, B, QUAD, P]),
+                    op=ALU.mult,
+                )
+            coef_of.pop(v)
 
         def add_up(v):
-            pair = [wave_of.pop(2 * v), wave_of.pop(2 * v + 1)]
+            wave = wave_of.pop(v)
             total = ps_sum.tile([P, B, P], F32)
             for b in range(B):
                 for t in range(2 * QUAD):
                     nc.tensor.matmul(
                         out=total[:, b, :],
-                        lhsT=pair[t // QUAD][:, b, (t % QUAD) * P : (t % QUAD + 1) * P],
+                        lhsT=wave[:, b, t * P : (t + 1) * P],
                         rhs=ident[:],
                         start=(t == 0),
                         stop=(t == 2 * QUAD - 1),
@@ -211,12 +233,13 @@ def tile_ka_attention_heads_mod_pa_kernel(
                     )
             total_of[v] = total
 
+        def load_shift(o):
+            shift_o = shifts.tile([P, G, P], BF16)
+            nc.sync.dma_start(out=shift_o[:], in_=shift_v[:, o : G * OUT_J : OUT_J, :])
+            shift_of[o] = shift_o
+
         def finish(v):
             o, j = divmod(v, G)
-            if j == 0:
-                shift_o = shifts.tile([P, G, P], BF16)
-                nc.sync.dma_start(out=shift_o[:], in_=shift_v[:, o : G * OUT_J : OUT_J, :])
-                shift_of[o] = shift_o
             res = results.tile([P, B, P], F32)
             nc.vector.tensor_tensor(
                 out=res[:],
@@ -227,19 +250,21 @@ def tile_ka_attention_heads_mod_pa_kernel(
             nc.sync.dma_start(out=out_v[:, :, j * OUT_J + o, :], in_=res[:])
 
         with tc.manual_schedule():
-            for u in range(2):
-                count_periods(u)
-                turn_coef(u)
+            load_shift(0)
+            count_periods(0)
+            count_periods(1)
+            turn_coef(0)
             sine(0)
-            for u in range(n_units):
-                if u + 2 < n_units:
-                    count_periods(u + 2)
-                    turn_coef(u + 2)
-                if u + 1 < n_units:
-                    sine(u + 1)
-                weigh(u)
-                if u % 2 == 1:
-                    add_up(u // 2)
-                    if u >= 3:
-                        finish(u // 2 - 1)
-            finish(n_units // 2 - 1)
+            for v in range(n_planes):
+                if v % G == 0 and v // G + 1 < OUT_J:
+                    load_shift(v // G + 1)
+                if v + 2 < n_planes:
+                    count_periods(v + 2)
+                if v + 1 < n_planes:
+                    turn_coef(v + 1)
+                    sine(v + 1)
+                weigh(v)
+                add_up(v)
+                if v >= 1:
+                    finish(v - 1)
+            finish(n_planes - 1)

@@ -140,44 +140,47 @@ def tile_ka_attention_heads_mod_pa_kernel(
 
         periods = whole.enter_context(tc.tile_pool(name="periods", bufs=2))
         waves = whole.enter_context(tc.tile_pool(name="waves", bufs=3))
-        shifts = whole.enter_context(tc.tile_pool(name="shifts", bufs=2))
+        shifts = whole.enter_context(tc.tile_pool(name="shifts", bufs=4))
         results = whole.enter_context(tc.tile_pool(name="results", bufs=3))
         ps_coef = whole.enter_context(tc.psum_pool(name="ps_coef", bufs=4))
         ps_sum = whole.enter_context(tc.psum_pool(name="ps_sum", bufs=2))
 
-        n_planes = OUT_J * G
+        n_planes = G * OUT_J
         k_of, coef_of, wave_of, total_of, shift_of = {}, {}, {}, {}, {}
 
         def quads(v):
-            o, j = divmod(v, G)
-            return [divmod(2 * o + half, CHUNKS // QUAD) for half in range(2)]
+            return [divmod(2 * (v % OUT_J) + half, CHUNKS // QUAD) for half in range(2)]
 
         def runs(v):
-            j = v % G
+            j = v // OUT_J
             (m0, cq0), (m1, cq1) = quads(v)
             pieces = [(m0, cq0, 0, 2)] if m0 == m1 else [(m0, cq0, 0, 1), (m1, cq1, 1, 1)]
-            found = []
-            for m, cq, first, n in pieces:
-                y0 = (j * CHUNKS + cq * QUAD) * P
-                found.append(
-                    (
-                        slice(first * QUAD * P, (first + n) * QUAD * P),
-                        xl[:, :, y0 : y0 + n * QUAD * P],
-                        turns[:, j * NF + m : j * NF + m + 1],
-                    )
+            return [
+                (
+                    slice(first * QUAD * P, (first + n) * QUAD * P),
+                    slice(cq * QUAD * P, (cq + n) * QUAD * P),
+                    j * NF + m,
                 )
-            return found
+                for m, cq, first, n in pieces
+            ]
 
-        def count_periods(v):
-            k = periods.tile([P, B, 2 * QUAD * P], I32)
-            for cols, xq, turn in runs(v):
-                nc.gpsimd.tensor_scalar(
-                    out=k[:, :, cols], in0=xq, scalar1=turn, scalar2=0.0, op0=ALU.mult, op1=ALU.add
-                )
-            k_of[v] = k
+        def x_of(j):
+            return xl[:, :, j * CHUNKS * P : (j + 1) * CHUNKS * P]
+
+        def count_periods(jm):
+            k = periods.tile([P, B, CHUNKS * P], I32)
+            nc.gpsimd.tensor_scalar(
+                out=k[:],
+                in0=x_of(jm // NF),
+                scalar1=turns[:, jm : jm + 1],
+                scalar2=0.0,
+                op0=ALU.mult,
+                op1=ALU.add,
+            )
+            k_of[jm] = k
 
         def turn_coef(v):
-            j = v % G
+            j = v // OUT_J
             coef_of[v] = []
             for m, cq in quads(v):
                 word = (m * G + j) // 2
@@ -190,14 +193,13 @@ def tile_ka_attention_heads_mod_pa_kernel(
                 coef_of[v].append(coef_t)
 
         def sine(v):
-            k = k_of.pop(v)
             wave = waves.tile([P, B, 2 * QUAD * P], F32)
-            for cols, xq, turn in runs(v):
+            for cols, x_cols, jm in runs(v):
                 nc.vector.scalar_tensor_tensor(
                     out=wave[:, :, cols],
-                    in0=xq,
-                    scalar=turn,
-                    in1=k[:, :, cols],
+                    in0=x_of(jm // NF)[:, :, x_cols],
+                    scalar=turns[:, jm : jm + 1],
+                    in1=k_of[jm][:, :, x_cols],
                     op0=ALU.mult,
                     op1=ALU.subtract,
                 )
@@ -205,7 +207,7 @@ def tile_ka_attention_heads_mod_pa_kernel(
             wave_of[v] = wave
 
         def weigh(v):
-            j = v % G
+            j = v // OUT_J
             for half, (m, cq) in enumerate(quads(v)):
                 pairs = coef_of[v][half][:].bitcast(BF16).rearrange("p c (q h) -> p c q h", h=2)
                 part = wave_of[v][:, :, half * QUAD * P : (half + 1) * QUAD * P]
@@ -216,16 +218,14 @@ def tile_ka_attention_heads_mod_pa_kernel(
                     in1=pairs[:, :, :, (m * G + j) % 2].unsqueeze(1).to_broadcast([P, B, QUAD, P]),
                     op=ALU.mult,
                 )
-            coef_of.pop(v)
 
         def add_up(v):
-            wave = wave_of.pop(v)
             total = ps_sum.tile([P, B, P], F32)
             for b in range(B):
                 for t in range(2 * QUAD):
                     nc.tensor.matmul(
                         out=total[:, b, :],
-                        lhsT=wave[:, b, t * P : (t + 1) * P],
+                        lhsT=wave_of[v][:, b, t * P : (t + 1) * P],
                         rhs=ident[:],
                         start=(t == 0),
                         stop=(t == 2 * QUAD - 1),
@@ -233,38 +233,35 @@ def tile_ka_attention_heads_mod_pa_kernel(
                     )
             total_of[v] = total
 
-        def load_shift(o):
-            shift_o = shifts.tile([P, G, P], BF16)
-            nc.sync.dma_start(out=shift_o[:], in_=shift_v[:, o : G * OUT_J : OUT_J, :])
-            shift_of[o] = shift_o
+        def load_shift(v):
+            shift_p = shifts.tile([P, P], BF16)
+            nc.sync.dma_start(out=shift_p[:], in_=shift_v[:, v, :])
+            shift_of[v] = shift_p
 
         def finish(v):
-            o, j = divmod(v, G)
             res = results.tile([P, B, P], F32)
             nc.vector.tensor_tensor(
                 out=res[:],
-                in0=total_of.pop(v)[:],
-                in1=shift_of[o][:, j, :].unsqueeze(1).to_broadcast([P, B, P]),
+                in0=total_of[v][:],
+                in1=shift_of[v][:].unsqueeze(1).to_broadcast([P, B, P]),
                 op=ALU.add,
             )
-            nc.sync.dma_start(out=out_v[:, :, j * OUT_J + o, :], in_=res[:])
+            nc.sync.dma_start(out=out_v[:, :, v, :], in_=res[:])
 
         with tc.manual_schedule():
+            counted = 0
             load_shift(0)
-            count_periods(0)
-            count_periods(1)
-            turn_coef(0)
-            sine(0)
-            for v in range(n_planes):
-                if v % G == 0 and v // G + 1 < OUT_J:
-                    load_shift(v // G + 1)
+            for v in range(-1, n_planes + 1):
                 if v + 2 < n_planes:
-                    count_periods(v + 2)
+                    load_shift(v + 2)
+                    while counted <= runs(v + 2)[-1][2]:
+                        count_periods(counted)
+                        counted += 1
                 if v + 1 < n_planes:
                     turn_coef(v + 1)
                     sine(v + 1)
-                weigh(v)
-                add_up(v)
+                if 0 <= v < n_planes:
+                    weigh(v)
+                    add_up(v)
                 if v >= 1:
                     finish(v - 1)
-            finish(n_planes - 1)

@@ -138,68 +138,68 @@ def tile_ka_attention_heads_mod_pa_kernel(
                         op=ALU.add,
                     )
 
-        periods = whole.enter_context(tc.tile_pool(name="periods", bufs=2))
+        periods = whole.enter_context(tc.tile_pool(name="periods", bufs=3))
         waves = whole.enter_context(tc.tile_pool(name="waves", bufs=3))
-        shifts = whole.enter_context(tc.tile_pool(name="shifts", bufs=4))
+        shifts = whole.enter_context(tc.tile_pool(name="shifts", bufs=2))
         results = whole.enter_context(tc.tile_pool(name="results", bufs=3))
         ps_coef = whole.enter_context(tc.psum_pool(name="ps_coef", bufs=4))
         ps_sum = whole.enter_context(tc.psum_pool(name="ps_sum", bufs=2))
 
-        n_planes = G * OUT_J
-        k_of, coef_of, wave_of, total_of, shift_of = {}, {}, {}, {}, {}
+        n_planes = OUT_J * G
+        k_of, coef_of, wave_of, total_of, shift_of, turned = {}, {}, {}, {}, {}, {}
 
         def quads(v):
-            return [divmod(2 * (v % OUT_J) + half, CHUNKS // QUAD) for half in range(2)]
+            o, j = divmod(v, G)
+            return [divmod(2 * o + half, CHUNKS // QUAD) for half in range(2)]
 
         def runs(v):
-            j = v // OUT_J
+            j = v % G
             (m0, cq0), (m1, cq1) = quads(v)
             pieces = [(m0, cq0, 0, 2)] if m0 == m1 else [(m0, cq0, 0, 1), (m1, cq1, 1, 1)]
-            return [
-                (
-                    slice(first * QUAD * P, (first + n) * QUAD * P),
-                    slice(cq * QUAD * P, (cq + n) * QUAD * P),
-                    j * NF + m,
+            found = []
+            for m, cq, first, n in pieces:
+                y0 = (j * CHUNKS + cq * QUAD) * P
+                found.append(
+                    (
+                        slice(first * QUAD * P, (first + n) * QUAD * P),
+                        xl[:, :, y0 : y0 + n * QUAD * P],
+                        turns[:, j * NF + m : j * NF + m + 1],
+                    )
                 )
-                for m, cq, first, n in pieces
-            ]
+            return found
 
-        def x_of(j):
-            return xl[:, :, j * CHUNKS * P : (j + 1) * CHUNKS * P]
-
-        def count_periods(jm):
-            k = periods.tile([P, B, CHUNKS * P], I32)
-            nc.gpsimd.tensor_scalar(
-                out=k[:],
-                in0=x_of(jm // NF),
-                scalar1=turns[:, jm : jm + 1],
-                scalar2=0.0,
-                op0=ALU.mult,
-                op1=ALU.add,
-            )
-            k_of[jm] = k
+        def count_periods(v):
+            k = periods.tile([P, B, 2 * QUAD * P], I32)
+            for cols, xq, turn in runs(v):
+                nc.gpsimd.tensor_scalar(
+                    out=k[:, :, cols], in0=xq, scalar1=turn, scalar2=0.0, op0=ALU.mult, op1=ALU.add
+                )
+            k_of[v] = k
 
         def turn_coef(v):
-            j = v // OUT_J
+            j = v % G
             coef_of[v] = []
-            for m, cq in quads(v):
+            for half, (m, cq) in enumerate(quads(v)):
                 word = (m * G + j) // 2
-                coef_t = ps_coef.tile([P, QUAD, P], F32)
-                for cl in range(QUAD):
-                    words = coef_sb[:, cq * QUAD + cl, :].bitcast(F32)
-                    nc.tensor.transpose(
-                        coef_t[:, cl, :], words[:, word : P * WORDS : WORDS], ident[:]
-                    )
-                coef_of[v].append(coef_t)
+                if turned.get(half, (None, None))[0] != (word, cq):
+                    coef_t = ps_coef.tile([P, QUAD, P], F32)
+                    for cl in range(QUAD):
+                        words = coef_sb[:, cq * QUAD + cl, :].bitcast(F32)
+                        nc.tensor.transpose(
+                            coef_t[:, cl, :], words[:, word : P * WORDS : WORDS], ident[:]
+                        )
+                    turned[half] = ((word, cq), coef_t)
+                coef_of[v].append(turned[half][1])
 
         def sine(v):
+            k = k_of.pop(v)
             wave = waves.tile([P, B, 2 * QUAD * P], F32)
-            for cols, x_cols, jm in runs(v):
+            for cols, xq, turn in runs(v):
                 nc.vector.scalar_tensor_tensor(
                     out=wave[:, :, cols],
-                    in0=x_of(jm // NF)[:, :, x_cols],
-                    scalar=turns[:, jm : jm + 1],
-                    in1=k_of[jm][:, :, x_cols],
+                    in0=xq,
+                    scalar=turn,
+                    in1=k[:, :, cols],
                     op0=ALU.mult,
                     op1=ALU.subtract,
                 )
@@ -207,7 +207,7 @@ def tile_ka_attention_heads_mod_pa_kernel(
             wave_of[v] = wave
 
         def weigh(v):
-            j = v // OUT_J
+            j = v % G
             for half, (m, cq) in enumerate(quads(v)):
                 pairs = coef_of[v][half][:].bitcast(BF16).rearrange("p c (q h) -> p c q h", h=2)
                 part = wave_of[v][:, :, half * QUAD * P : (half + 1) * QUAD * P]
@@ -218,14 +218,16 @@ def tile_ka_attention_heads_mod_pa_kernel(
                     in1=pairs[:, :, :, (m * G + j) % 2].unsqueeze(1).to_broadcast([P, B, QUAD, P]),
                     op=ALU.mult,
                 )
+            coef_of.pop(v)
 
         def add_up(v):
+            wave = wave_of.pop(v)
             total = ps_sum.tile([P, B, P], F32)
             for b in range(B):
                 for t in range(2 * QUAD):
                     nc.tensor.matmul(
                         out=total[:, b, :],
-                        lhsT=wave_of[v][:, b, t * P : (t + 1) * P],
+                        lhsT=wave[:, b, t * P : (t + 1) * P],
                         rhs=ident[:],
                         start=(t == 0),
                         stop=(t == 2 * QUAD - 1),
@@ -233,35 +235,39 @@ def tile_ka_attention_heads_mod_pa_kernel(
                     )
             total_of[v] = total
 
-        def load_shift(v):
-            shift_p = shifts.tile([P, P], BF16)
-            nc.sync.dma_start(out=shift_p[:], in_=shift_v[:, v, :])
-            shift_of[v] = shift_p
+        def load_shift(o):
+            shift_o = shifts.tile([P, G, P], BF16)
+            nc.sync.dma_start(out=shift_o[:], in_=shift_v[:, o : G * OUT_J : OUT_J, :])
+            shift_of[o] = shift_o
 
         def finish(v):
+            o, j = divmod(v, G)
             res = results.tile([P, B, P], F32)
             nc.vector.tensor_tensor(
                 out=res[:],
-                in0=total_of[v][:],
-                in1=shift_of[v][:].unsqueeze(1).to_broadcast([P, B, P]),
+                in0=total_of.pop(v)[:],
+                in1=shift_of[o][:, j, :].unsqueeze(1).to_broadcast([P, B, P]),
                 op=ALU.add,
             )
-            nc.sync.dma_start(out=out_v[:, :, v, :], in_=res[:])
+            nc.sync.dma_start(out=out_v[:, :, j * OUT_J + o, :], in_=res[:])
 
         with tc.manual_schedule():
-            counted = 0
             load_shift(0)
-            for v in range(-1, n_planes + 1):
-                if v + 2 < n_planes:
-                    load_shift(v + 2)
-                    while counted <= runs(v + 2)[-1][2]:
-                        count_periods(counted)
-                        counted += 1
+            count_periods(0)
+            count_periods(1)
+            count_periods(2)
+            turn_coef(0)
+            sine(0)
+            for v in range(n_planes):
+                if v % G == 0 and v // G + 1 < OUT_J:
+                    load_shift(v // G + 1)
+                if v + 3 < n_planes:
+                    count_periods(v + 3)
                 if v + 1 < n_planes:
                     turn_coef(v + 1)
                     sine(v + 1)
-                if 0 <= v < n_planes:
-                    weigh(v)
-                    add_up(v)
+                weigh(v)
+                add_up(v)
                 if v >= 1:
                     finish(v - 1)
+            finish(n_planes - 1)

@@ -29,6 +29,9 @@ OUT_J = QUADS_J // 2
 PLANES = NF * G
 WORDS = PLANES // 2
 TWO_PI = 2.0 * math.pi
+QUADS_M = CHUNKS // QUAD
+NPE = (2, 1, 1)
+OFFSET = 12582912.0
 
 FLOPS = 2 * ROWS * D * COLS
 
@@ -138,43 +141,110 @@ def tile_ka_attention_heads_mod_pa_kernel(
                         op=ALU.add,
                     )
 
-        periods = whole.enter_context(tc.tile_pool(name="periods", bufs=3))
+            for j in range(G):
+                for cq in range(QUADS_M):
+                    y0 = (j * CHUNKS + cq * QUAD) * P
+                    mm = ps_mm.tile([P, B, NPE[cq] * P], F32)
+                    for b in range(B):
+                        for cl in range(NPE[cq]):
+                            nc.tensor.transpose(
+                                mm[:, b, cl * P : (cl + 1) * P],
+                                xl[:, b, y0 + cl * P : y0 + (cl + 1) * P],
+                                ident[:],
+                            )
+                    nc.scalar.copy(out=xl[:, :, y0 : y0 + NPE[cq] * P], in_=mm[:])
+
+        periods = whole.enter_context(tc.tile_pool(name="periods", bufs=2))
+        scaled = whole.enter_context(tc.tile_pool(name="scaled", bufs=2))
+        marks = whole.enter_context(tc.tile_pool(name="marks", bufs=1))
+        backs = whole.enter_context(tc.tile_pool(name="backs", bufs=2))
         waves = whole.enter_context(tc.tile_pool(name="waves", bufs=3))
         shifts = whole.enter_context(tc.tile_pool(name="shifts", bufs=2))
         results = whole.enter_context(tc.tile_pool(name="results", bufs=3))
         ps_coef = whole.enter_context(tc.psum_pool(name="ps_coef", bufs=4))
-        ps_sum = whole.enter_context(tc.psum_pool(name="ps_sum", bufs=2))
+        ps_frac = whole.enter_context(tc.psum_pool(name="ps_frac", bufs=3))
+        ps_sum = whole.enter_context(tc.psum_pool(name="ps_sum", bufs=1))
 
         n_planes = OUT_J * G
-        k_of, coef_of, wave_of, total_of, shift_of, turned = {}, {}, {}, {}, {}, {}
+        k_of, t_of, back_of, frac_of, coef_of, wave_of, total_of, shift_of, turned = (
+            {}, {}, {}, {}, {}, {}, {}, {}, {},
+        )
 
         def quads(v):
             o, j = divmod(v, G)
-            return [divmod(2 * o + half, CHUNKS // QUAD) for half in range(2)]
+            return [divmod(2 * o + half, QUADS_M) for half in range(2)]
 
-        def runs(v):
+        def parts(v):
             j = v % G
-            (m0, cq0), (m1, cq1) = quads(v)
-            pieces = [(m0, cq0, 0, 2)] if m0 == m1 else [(m0, cq0, 0, 1), (m1, cq1, 1, 1)]
-            found = []
-            for m, cq, first, n in pieces:
-                y0 = (j * CHUNKS + cq * QUAD) * P
+            found, n_t, n_v = [], 0, 0
+            for m, cq in quads(v):
                 found.append(
                     (
-                        slice(first * QUAD * P, (first + n) * QUAD * P),
-                        xl[:, :, y0 : y0 + n * QUAD * P],
                         turns[:, j * NF + m : j * NF + m + 1],
+                        (j * CHUNKS + cq * QUAD) * P,
+                        NPE[cq] * P,
+                        n_t,
+                        n_v,
                     )
                 )
-            return found
+                n_t += NPE[cq] * P
+                n_v += (QUAD - NPE[cq]) * P
+            return found, n_t, n_v
 
         def count_periods(v):
-            k = periods.tile([P, B, 2 * QUAD * P], I32)
-            for cols, xq, turn in runs(v):
+            found, n_t, n_v = parts(v)
+            k = periods.tile([P, B, n_v], I32)
+            for turn, y0, split, at_t, at_v in found:
                 nc.gpsimd.tensor_scalar(
-                    out=k[:, :, cols], in0=xq, scalar1=turn, scalar2=0.0, op0=ALU.mult, op1=ALU.add
+                    out=k[:, :, at_v : at_v + QUAD * P - split],
+                    in0=xl[:, :, y0 + split : y0 + QUAD * P],
+                    scalar1=turn,
+                    scalar2=0.0,
+                    op0=ALU.mult,
+                    op1=ALU.add,
                 )
             k_of[v] = k
+
+        def scale_up(v):
+            found, n_t, n_v = parts(v)
+            t = scaled.tile([P, B, n_t], F32)
+            for turn, y0, split, at_t, at_v in found:
+                nc.gpsimd.tensor_scalar(
+                    out=t[:, :, at_t : at_t + split],
+                    in0=xl[:, :, y0 : y0 + split],
+                    scalar1=turn,
+                    scalar2=0.0,
+                    op0=ALU.mult,
+                    op1=ALU.add,
+                )
+            t_of[v] = t
+
+        def round_off(v):
+            found, n_t, n_v = parts(v)
+            mark = marks.tile([P, B, n_t], U32)
+            back = backs.tile([P, B, n_t], F32)
+            nc.scalar.activation(out=mark[:], in_=t_of[v][:], func=ACT.Copy, scale=1.0, bias=OFFSET)
+            nc.scalar.activation(out=back[:], in_=mark[:], func=ACT.Copy, scale=-1.0, bias=OFFSET)
+            back_of[v] = back
+
+        def take_off(v):
+            found, n_t, n_v = parts(v)
+            t, back = t_of.pop(v), back_of.pop(v)
+            frac_of[v] = []
+            for turn, y0, split, at_t, at_v in found:
+                frac = ps_frac.tile([P, B, split], F32)
+                for b in range(B):
+                    for c0 in range(0, split, P):
+                        for step, src in enumerate((t, back)):
+                            nc.tensor.matmul(
+                                out=frac[:, b, c0 : c0 + P],
+                                lhsT=src[:, b, at_t + c0 : at_t + c0 + P],
+                                rhs=ident[:],
+                                start=(step == 0),
+                                stop=(step == 1),
+                                is_transpose=True,
+                            )
+                frac_of[v].append(frac)
 
         def turn_coef(v):
             j = v % G
@@ -191,37 +261,54 @@ def tile_ka_attention_heads_mod_pa_kernel(
                     turned[half] = ((word, cq), coef_t)
                 coef_of[v].append(turned[half][1])
 
-        def sine(v):
+        def subtract(v):
+            found, n_t, n_v = parts(v)
             k = k_of.pop(v)
             wave = waves.tile([P, B, 2 * QUAD * P], F32)
-            for cols, xq, turn in runs(v):
+            for half, (turn, y0, split, at_t, at_v) in enumerate(found):
                 nc.vector.scalar_tensor_tensor(
-                    out=wave[:, :, cols],
-                    in0=xq,
+                    out=wave[:, :, half * QUAD * P + split : (half + 1) * QUAD * P],
+                    in0=xl[:, :, y0 + split : y0 + QUAD * P],
                     scalar=turn,
-                    in1=k[:, :, cols],
+                    in1=k[:, :, at_v : at_v + QUAD * P - split],
                     op0=ALU.mult,
                     op1=ALU.subtract,
                 )
-            nc.scalar.activation(out=wave[:], in_=wave[:], func=ACT.Sin, scale=TWO_PI)
             wave_of[v] = wave
 
-        def weigh(v):
-            j = v % G
-            for half, (m, cq) in enumerate(quads(v)):
-                pairs = coef_of[v][half][:].bitcast(BF16).rearrange("p c (q h) -> p c q h", h=2)
-                part = wave_of[v][:, :, half * QUAD * P : (half + 1) * QUAD * P]
-                part = part.rearrange("p b (c q) -> p b c q", c=QUAD)
-                nc.vector.tensor_tensor(
-                    out=part,
-                    in0=part,
-                    in1=pairs[:, :, :, (m * G + j) % 2].unsqueeze(1).to_broadcast([P, B, QUAD, P]),
-                    op=ALU.mult,
+        def sine_tensor_way(v):
+            found, n_t, n_v = parts(v)
+            for half, (turn, y0, split, at_t, at_v) in enumerate(found):
+                nc.scalar.activation(
+                    out=wave_of[v][:, :, half * QUAD * P : half * QUAD * P + split],
+                    in_=frac_of[v][half][:],
+                    func=ACT.Sin,
+                    scale=TWO_PI,
                 )
-            coef_of.pop(v)
+            frac_of.pop(v)
+
+        def sine_vector_way(v):
+            found, n_t, n_v = parts(v)
+            for half, (turn, y0, split, at_t, at_v) in enumerate(found):
+                rest = wave_of[v][:, :, half * QUAD * P + split : (half + 1) * QUAD * P]
+                nc.scalar.activation(out=rest, in_=rest, func=ACT.Sin, scale=TWO_PI)
+
+        def weigh(v, half):
+            j = v % G
+            m, cq = quads(v)[half]
+            pairs = coef_of[v][half][:].bitcast(BF16).rearrange("p c (q h) -> p c q h", h=2)
+            part = wave_of[v][:, :, half * QUAD * P : (half + 1) * QUAD * P]
+            part = part.rearrange("p b (c q) -> p b c q", c=QUAD)
+            nc.vector.tensor_tensor(
+                out=part,
+                in0=part,
+                in1=pairs[:, :, :, (m * G + j) % 2].unsqueeze(1).to_broadcast([P, B, QUAD, P]),
+                op=ALU.mult,
+            )
 
         def add_up(v):
             wave = wave_of.pop(v)
+            coef_of.pop(v)
             total = ps_sum.tile([P, B, P], F32)
             for b in range(B):
                 for t in range(2 * QUAD):
@@ -254,20 +341,40 @@ def tile_ka_attention_heads_mod_pa_kernel(
         with tc.manual_schedule():
             load_shift(0)
             count_periods(0)
+            scale_up(0)
+            scale_up(1)
             count_periods(1)
-            count_periods(2)
+            round_off(0)
+            take_off(0)
+            round_off(1)
+            subtract(0)
+            sine_tensor_way(0)
+            sine_vector_way(0)
             turn_coef(0)
-            sine(0)
+            take_off(1)
+            count_periods(2)
+            scale_up(2)
             for v in range(n_planes):
                 if v % G == 0 and v // G + 1 < OUT_J:
                     load_shift(v // G + 1)
+                if v >= 1:
+                    add_up(v - 1)
+                if v + 2 < n_planes:
+                    round_off(v + 2)
+                if v + 1 < n_planes:
+                    subtract(v + 1)
                 if v + 3 < n_planes:
                     count_periods(v + 3)
+                    scale_up(v + 3)
                 if v + 1 < n_planes:
+                    sine_tensor_way(v + 1)
                     turn_coef(v + 1)
-                    sine(v + 1)
-                weigh(v)
-                add_up(v)
+                    sine_vector_way(v + 1)
+                weigh(v, 0)
                 if v >= 1:
                     finish(v - 1)
+                weigh(v, 1)
+                if v + 2 < n_planes:
+                    take_off(v + 2)
+            add_up(n_planes - 1)
             finish(n_planes - 1)

@@ -30,7 +30,9 @@ PLANES = NF * G
 WORDS = PLANES // 2
 TWO_PI = 2.0 * math.pi
 QUADS_M = CHUNKS // QUAD
-NPE = (2, 1, 1)
+QW = QUAD * P
+TW = P
+VW = QW - TW
 OFFSET = 12582912.0
 
 FLOPS = 2 * ROWS * D * COLS
@@ -142,17 +144,13 @@ def tile_ka_attention_heads_mod_pa_kernel(
                     )
 
             for j in range(G):
-                for cq in range(QUADS_M):
-                    y0 = (j * CHUNKS + cq * QUAD) * P
-                    mm = ps_mm.tile([P, B, NPE[cq] * P], F32)
-                    for b in range(B):
-                        for cl in range(NPE[cq]):
-                            nc.tensor.transpose(
-                                mm[:, b, cl * P : (cl + 1) * P],
-                                xl[:, b, y0 + cl * P : y0 + (cl + 1) * P],
-                                ident[:],
-                            )
-                    nc.scalar.copy(out=xl[:, :, y0 : y0 + NPE[cq] * P], in_=mm[:])
+                for b in range(B):
+                    group = xl[:, b, j * CHUNKS * P : (j + 1) * CHUNKS * P]
+                    firsts = group.rearrange("p (s c) -> p s c", c=QW)[:, :, 0:TW]
+                    mm = ps_mm.tile([P, QUADS_M, TW], F32)
+                    for cq in range(QUADS_M):
+                        nc.tensor.transpose(mm[:, cq, :], firsts[:, cq, :], ident[:])
+                    nc.scalar.copy(out=firsts, in_=mm[:])
 
         periods = whole.enter_context(tc.tile_pool(name="periods", bufs=2))
         scaled = whole.enter_context(tc.tile_pool(name="scaled", bufs=2))
@@ -162,8 +160,8 @@ def tile_ka_attention_heads_mod_pa_kernel(
         shifts = whole.enter_context(tc.tile_pool(name="shifts", bufs=2))
         results = whole.enter_context(tc.tile_pool(name="results", bufs=3))
         ps_coef = whole.enter_context(tc.psum_pool(name="ps_coef", bufs=4))
-        ps_frac = whole.enter_context(tc.psum_pool(name="ps_frac", bufs=3))
-        ps_sum = whole.enter_context(tc.psum_pool(name="ps_sum", bufs=1))
+        ps_frac = whole.enter_context(tc.psum_pool(name="ps_frac", bufs=2))
+        ps_sum = whole.enter_context(tc.psum_pool(name="ps_sum", bufs=2))
 
         n_planes = OUT_J * G
         k_of, t_of, back_of, frac_of, coef_of, wave_of, total_of, shift_of, turned = (
@@ -174,30 +172,29 @@ def tile_ka_attention_heads_mod_pa_kernel(
             o, j = divmod(v, G)
             return [divmod(2 * o + half, QUADS_M) for half in range(2)]
 
-        def parts(v):
+        def runs(v):
             j = v % G
-            found, n_t, n_v = [], 0, 0
-            for m, cq in quads(v):
+            (m0, cq0), (m1, cq1) = quads(v)
+            pieces = [(0, 2, m0, cq0)] if m0 == m1 else [(0, 1, m0, cq0), (1, 1, m1, cq1)]
+            found = []
+            for first, n, m, cq in pieces:
+                y0 = (j * CHUNKS + cq * QUAD) * P
                 found.append(
                     (
+                        first,
+                        n,
+                        xl[:, :, y0 : y0 + n * QW].rearrange("p b (h c) -> p b h c", c=QW),
                         turns[:, j * NF + m : j * NF + m + 1],
-                        (j * CHUNKS + cq * QUAD) * P,
-                        NPE[cq] * P,
-                        n_t,
-                        n_v,
                     )
                 )
-                n_t += NPE[cq] * P
-                n_v += (QUAD - NPE[cq]) * P
-            return found, n_t, n_v
+            return found
 
         def count_periods(v):
-            found, n_t, n_v = parts(v)
-            k = periods.tile([P, B, n_v], I32)
-            for turn, y0, split, at_t, at_v in found:
+            k = periods.tile([P, B, 2, VW], I32)
+            for first, n, xq, turn in runs(v):
                 nc.gpsimd.tensor_scalar(
-                    out=k[:, :, at_v : at_v + QUAD * P - split],
-                    in0=xl[:, :, y0 + split : y0 + QUAD * P],
+                    out=k[:, :, first : first + n, :],
+                    in0=xq[:, :, :, TW:QW],
                     scalar1=turn,
                     scalar2=0.0,
                     op0=ALU.mult,
@@ -205,46 +202,34 @@ def tile_ka_attention_heads_mod_pa_kernel(
                 )
             k_of[v] = k
 
-        def scale_up(v):
-            found, n_t, n_v = parts(v)
-            t = scaled.tile([P, B, n_t], F32)
-            for turn, y0, split, at_t, at_v in found:
-                nc.gpsimd.tensor_scalar(
-                    out=t[:, :, at_t : at_t + split],
-                    in0=xl[:, :, y0 : y0 + split],
-                    scalar1=turn,
-                    scalar2=0.0,
-                    op0=ALU.mult,
-                    op1=ALU.add,
-                )
-            t_of[v] = t
-
         def round_off(v):
-            found, n_t, n_v = parts(v)
-            mark = marks.tile([P, B, n_t], U32)
-            back = backs.tile([P, B, n_t], F32)
-            nc.scalar.activation(out=mark[:], in_=t_of[v][:], func=ACT.Copy, scale=1.0, bias=OFFSET)
+            t = scaled.tile([P, B, 2, TW], F32)
+            mark = marks.tile([P, B, 2, TW], U32)
+            back = backs.tile([P, B, 2, TW], F32)
+            for first, n, xq, turn in runs(v):
+                nc.scalar.activation(
+                    out=t[:, :, first : first + n, :], in_=xq[:, :, :, 0:TW], func=ACT.Copy, scale=turn
+                )
+            nc.scalar.activation(out=mark[:], in_=t[:], func=ACT.Copy, scale=1.0, bias=OFFSET)
             nc.scalar.activation(out=back[:], in_=mark[:], func=ACT.Copy, scale=-1.0, bias=OFFSET)
+            t_of[v] = t
             back_of[v] = back
 
         def take_off(v):
-            found, n_t, n_v = parts(v)
             t, back = t_of.pop(v), back_of.pop(v)
-            frac_of[v] = []
-            for turn, y0, split, at_t, at_v in found:
-                frac = ps_frac.tile([P, B, split], F32)
-                for b in range(B):
-                    for c0 in range(0, split, P):
-                        for step, src in enumerate((t, back)):
-                            nc.tensor.matmul(
-                                out=frac[:, b, c0 : c0 + P],
-                                lhsT=src[:, b, at_t + c0 : at_t + c0 + P],
-                                rhs=ident[:],
-                                start=(step == 0),
-                                stop=(step == 1),
-                                is_transpose=True,
-                            )
-                frac_of[v].append(frac)
+            frac = ps_frac.tile([P, B, 2, TW], F32)
+            for b in range(B):
+                for half in range(2):
+                    for step, src in enumerate((t, back)):
+                        nc.tensor.matmul(
+                            out=frac[:, b, half, :],
+                            lhsT=src[:, b, half, :],
+                            rhs=ident[:],
+                            start=(step == 0),
+                            stop=(step == 1),
+                            is_transpose=True,
+                        )
+            frac_of[v] = frac
 
         def turn_coef(v):
             j = v % G
@@ -262,43 +247,34 @@ def tile_ka_attention_heads_mod_pa_kernel(
                 coef_of[v].append(turned[half][1])
 
         def subtract(v):
-            found, n_t, n_v = parts(v)
             k = k_of.pop(v)
-            wave = waves.tile([P, B, 2 * QUAD * P], F32)
-            for half, (turn, y0, split, at_t, at_v) in enumerate(found):
-                nc.vector.scalar_tensor_tensor(
-                    out=wave[:, :, half * QUAD * P + split : (half + 1) * QUAD * P],
-                    in0=xl[:, :, y0 + split : y0 + QUAD * P],
-                    scalar=turn,
-                    in1=k[:, :, at_v : at_v + QUAD * P - split],
-                    op0=ALU.mult,
-                    op1=ALU.subtract,
-                )
+            wave = waves.tile([P, B, 2, QW], F32)
+            for first, n, xq, turn in runs(v):
+                for h in range(n):
+                    nc.vector.scalar_tensor_tensor(
+                        out=wave[:, :, first + h, TW:QW],
+                        in0=xq[:, :, h, TW:QW],
+                        scalar=turn,
+                        in1=k[:, :, first + h, :],
+                        op0=ALU.mult,
+                        op1=ALU.subtract,
+                    )
             wave_of[v] = wave
 
         def sine_tensor_way(v):
-            found, n_t, n_v = parts(v)
-            for half, (turn, y0, split, at_t, at_v) in enumerate(found):
-                nc.scalar.activation(
-                    out=wave_of[v][:, :, half * QUAD * P : half * QUAD * P + split],
-                    in_=frac_of[v][half][:],
-                    func=ACT.Sin,
-                    scale=TWO_PI,
-                )
-            frac_of.pop(v)
+            nc.scalar.activation(
+                out=wave_of[v][:, :, :, 0:TW], in_=frac_of.pop(v)[:], func=ACT.Sin, scale=TWO_PI
+            )
 
         def sine_vector_way(v):
-            found, n_t, n_v = parts(v)
-            for half, (turn, y0, split, at_t, at_v) in enumerate(found):
-                rest = wave_of[v][:, :, half * QUAD * P + split : (half + 1) * QUAD * P]
-                nc.scalar.activation(out=rest, in_=rest, func=ACT.Sin, scale=TWO_PI)
+            rest = wave_of[v][:, :, :, TW:QW]
+            nc.scalar.activation(out=rest, in_=rest, func=ACT.Sin, scale=TWO_PI)
 
         def weigh(v, half):
             j = v % G
             m, cq = quads(v)[half]
             pairs = coef_of[v][half][:].bitcast(BF16).rearrange("p c (q h) -> p c q h", h=2)
-            part = wave_of[v][:, :, half * QUAD * P : (half + 1) * QUAD * P]
-            part = part.rearrange("p b (c q) -> p b c q", c=QUAD)
+            part = wave_of[v][:, :, half, :].rearrange("p b (c q) -> p b c q", c=QUAD)
             nc.vector.tensor_tensor(
                 out=part,
                 in0=part,
@@ -312,9 +288,10 @@ def tile_ka_attention_heads_mod_pa_kernel(
             total = ps_sum.tile([P, B, P], F32)
             for b in range(B):
                 for t in range(2 * QUAD):
+                    half, cl = divmod(t, QUAD)
                     nc.tensor.matmul(
                         out=total[:, b, :],
-                        lhsT=wave[:, b, t * P : (t + 1) * P],
+                        lhsT=wave[:, b, half, cl * P : (cl + 1) * P],
                         rhs=ident[:],
                         start=(t == 0),
                         stop=(t == 2 * QUAD - 1),
@@ -341,8 +318,6 @@ def tile_ka_attention_heads_mod_pa_kernel(
         with tc.manual_schedule():
             load_shift(0)
             count_periods(0)
-            scale_up(0)
-            scale_up(1)
             count_periods(1)
             round_off(0)
             take_off(0)
@@ -353,7 +328,6 @@ def tile_ka_attention_heads_mod_pa_kernel(
             turn_coef(0)
             take_off(1)
             count_periods(2)
-            scale_up(2)
             for v in range(n_planes):
                 if v % G == 0 and v // G + 1 < OUT_J:
                     load_shift(v // G + 1)
@@ -365,7 +339,6 @@ def tile_ka_attention_heads_mod_pa_kernel(
                     subtract(v + 1)
                 if v + 3 < n_planes:
                     count_periods(v + 3)
-                    scale_up(v + 3)
                 if v + 1 < n_planes:
                     sine_tensor_way(v + 1)
                     turn_coef(v + 1)

@@ -233,18 +233,23 @@ def tile_ka_attention_heads_mod_pa_kernel(
 
         def turn_coef(v):
             j = v % G
+            fresh = {}
             coef_of[v] = []
-            for half, (m, cq) in enumerate(quads(v)):
-                word = (m * G + j) // 2
-                if turned.get(half, (None, None))[0] != (word, cq):
+            for m, cq in quads(v):
+                key = ((m * G + j) // 2, cq)
+                coef_t = turned.get(key)
+                if coef_t is None:
                     coef_t = ps_coef.tile([P, QUAD, P], F32)
                     for cl in range(QUAD):
                         words = coef_sb[:, cq * QUAD + cl, :].bitcast(F32)
                         nc.tensor.transpose(
-                            coef_t[:, cl, :], words[:, word : P * WORDS : WORDS], ident[:]
+                            coef_t[:, cl, :], words[:, key[0] : P * WORDS : WORDS], ident[:]
                         )
-                    turned[half] = ((word, cq), coef_t)
-                coef_of[v].append(turned[half][1])
+                fresh[key] = coef_t
+                coef_of[v].append(coef_t)
+            turned.clear()
+            for key in fresh:
+                turned[key] = fresh[key]
 
         def subtract(v):
             k = k_of.pop(v)

@@ -153,9 +153,9 @@ def tile_ka_attention_heads_mod_pa_kernel(
                     nc.scalar.copy(out=firsts, in_=mm[:])
 
         periods = whole.enter_context(tc.tile_pool(name="periods", bufs=2))
-        scaled = whole.enter_context(tc.tile_pool(name="scaled", bufs=2))
+        scaled = whole.enter_context(tc.tile_pool(name="scaled", bufs=3))
         marks = whole.enter_context(tc.tile_pool(name="marks", bufs=1))
-        backs = whole.enter_context(tc.tile_pool(name="backs", bufs=2))
+        backs = whole.enter_context(tc.tile_pool(name="backs", bufs=3))
         waves = whole.enter_context(tc.tile_pool(name="waves", bufs=3))
         shifts = whole.enter_context(tc.tile_pool(name="shifts", bufs=2))
         results = whole.enter_context(tc.tile_pool(name="results", bufs=3))
@@ -164,8 +164,8 @@ def tile_ka_attention_heads_mod_pa_kernel(
         ps_sum = whole.enter_context(tc.psum_pool(name="ps_sum", bufs=2))
 
         n_planes = OUT_J * G
-        k_of, t_of, back_of, frac_of, coef_of, wave_of, total_of, shift_of, turned = (
-            {}, {}, {}, {}, {}, {}, {}, {}, {},
+        k_of, t_of, mark_of, back_of, frac_of, coef_of, wave_of, total_of, shift_of, turned = (
+            {}, {}, {}, {}, {}, {}, {}, {}, {}, {},
         )
 
         def quads(v):
@@ -202,17 +202,24 @@ def tile_ka_attention_heads_mod_pa_kernel(
                 )
             k_of[v] = k
 
-        def round_off(v):
+        def scale_up(v):
             t = scaled.tile([P, B, 2, TW], F32)
-            mark = marks.tile([P, B, 2, TW], U32)
-            back = backs.tile([P, B, 2, TW], F32)
             for first, n, xq, turn in runs(v):
                 nc.scalar.activation(
                     out=t[:, :, first : first + n, :], in_=xq[:, :, :, 0:TW], func=ACT.Copy, scale=turn
                 )
-            nc.scalar.activation(out=mark[:], in_=t[:], func=ACT.Copy, scale=1.0, bias=OFFSET)
-            nc.scalar.activation(out=back[:], in_=mark[:], func=ACT.Copy, scale=-1.0, bias=OFFSET)
             t_of[v] = t
+
+        def round_off(v):
+            mark = marks.tile([P, B, 2, TW], U32)
+            nc.scalar.activation(out=mark[:], in_=t_of[v][:], func=ACT.Copy, scale=1.0, bias=OFFSET)
+            mark_of[v] = mark
+
+        def negate(v):
+            back = backs.tile([P, B, 2, TW], F32)
+            nc.scalar.activation(
+                out=back[:], in_=mark_of.pop(v)[:], func=ACT.Copy, scale=-1.0, bias=OFFSET
+            )
             back_of[v] = back
 
         def take_off(v):
@@ -324,22 +331,29 @@ def tile_ka_attention_heads_mod_pa_kernel(
             load_shift(0)
             count_periods(0)
             count_periods(1)
+            scale_up(0)
+            scale_up(1)
             round_off(0)
-            take_off(0)
+            negate(0)
             round_off(1)
+            negate(1)
+            take_off(0)
             subtract(0)
             sine_tensor_way(0)
             sine_vector_way(0)
             turn_coef(0)
             take_off(1)
             count_periods(2)
+            scale_up(2)
+            round_off(2)
+            negate(2)
             for v in range(n_planes):
                 if v % G == 0 and v // G + 1 < OUT_J:
                     load_shift(v // G + 1)
                 if v >= 1:
                     add_up(v - 1)
-                if v + 2 < n_planes:
-                    round_off(v + 2)
+                if v + 3 < n_planes:
+                    scale_up(v + 3)
                 if v + 1 < n_planes:
                     subtract(v + 1)
                 if v + 3 < n_planes:
@@ -347,7 +361,12 @@ def tile_ka_attention_heads_mod_pa_kernel(
                 if v + 1 < n_planes:
                     sine_tensor_way(v + 1)
                     turn_coef(v + 1)
+                if v + 3 < n_planes:
+                    round_off(v + 3)
+                if v + 1 < n_planes:
                     sine_vector_way(v + 1)
+                if v + 3 < n_planes:
+                    negate(v + 3)
                 weigh(v, 0)
                 if v >= 1:
                     finish(v - 1)

@@ -154,19 +154,21 @@ def tile_ka_attention_heads_mod_pa_kernel(
 
         periods = whole.enter_context(tc.tile_pool(name="periods", bufs=2))
         scaled = whole.enter_context(tc.tile_pool(name="scaled", bufs=3))
-        marks = whole.enter_context(tc.tile_pool(name="marks", bufs=1))
-        backs = whole.enter_context(tc.tile_pool(name="backs", bufs=3))
+        marks = whole.enter_context(tc.tile_pool(name="marks", bufs=2))
+        backs = whole.enter_context(tc.tile_pool(name="backs", bufs=2))
         waves = whole.enter_context(tc.tile_pool(name="waves", bufs=3))
         shifts = whole.enter_context(tc.tile_pool(name="shifts", bufs=2))
         results = whole.enter_context(tc.tile_pool(name="results", bufs=3))
         ps_coef = whole.enter_context(tc.psum_pool(name="ps_coef", bufs=4))
         ps_frac = whole.enter_context(tc.psum_pool(name="ps_frac", bufs=2))
-        ps_sum = whole.enter_context(tc.psum_pool(name="ps_sum", bufs=2))
+        ps_sum = whole.enter_context(tc.psum_pool(name="ps_sum", bufs=1))
+        ps_hold = whole.enter_context(tc.psum_pool(name="ps_hold", bufs=1))
 
         n_planes = OUT_J * G
         k_of, t_of, mark_of, back_of, frac_of, coef_of, wave_of, total_of, shift_of, turned = (
             {}, {}, {}, {}, {}, {}, {}, {}, {}, {},
         )
+        held = {}
 
         def quads(v):
             o, j = divmod(v, G)
@@ -244,14 +246,18 @@ def tile_ka_attention_heads_mod_pa_kernel(
             coef_of[v] = []
             for m, cq in quads(v):
                 key = ((m * G + j) // 2, cq)
-                coef_t = turned.get(key)
+                far = cq == 1 and m % 2 == 0 and j == G - 1
+                coef_t = held.pop(key) if key in held else turned.get(key)
                 if coef_t is None:
-                    coef_t = ps_coef.tile([P, QUAD, P], F32)
+                    pool = ps_hold if far else ps_coef
+                    coef_t = pool.tile([P, QUAD, P], F32)
                     for cl in range(QUAD):
                         words = coef_sb[:, cq * QUAD + cl, :].bitcast(F32)
                         nc.tensor.transpose(
                             coef_t[:, cl, :], words[:, key[0] : P * WORDS : WORDS], ident[:]
                         )
+                    if far:
+                        held[key] = coef_t
                 fresh[key] = coef_t
                 coef_of[v].append(coef_t)
             turned.clear()
@@ -337,23 +343,27 @@ def tile_ka_attention_heads_mod_pa_kernel(
             negate(0)
             round_off(1)
             negate(1)
+            scale_up(2)
             take_off(0)
             subtract(0)
             sine_tensor_way(0)
+            round_off(2)
             sine_vector_way(0)
             turn_coef(0)
             take_off(1)
             count_periods(2)
-            scale_up(2)
-            round_off(2)
-            negate(2)
+            scale_up(3)
             for v in range(n_planes):
                 if v % G == 0 and v // G + 1 < OUT_J:
                     load_shift(v // G + 1)
                 if v >= 1:
                     add_up(v - 1)
+                if v + 2 < n_planes:
+                    negate(v + 2)
                 if v + 3 < n_planes:
-                    scale_up(v + 3)
+                    round_off(v + 3)
+                if v + 4 < n_planes:
+                    scale_up(v + 4)
                 if v + 1 < n_planes:
                     subtract(v + 1)
                 if v + 3 < n_planes:
@@ -361,12 +371,7 @@ def tile_ka_attention_heads_mod_pa_kernel(
                 if v + 1 < n_planes:
                     sine_tensor_way(v + 1)
                     turn_coef(v + 1)
-                if v + 3 < n_planes:
-                    round_off(v + 3)
-                if v + 1 < n_planes:
                     sine_vector_way(v + 1)
-                if v + 3 < n_planes:
-                    negate(v + 3)
                 weigh(v, 0)
                 if v >= 1:
                     finish(v - 1)

@@ -33,6 +33,8 @@ QUADS_M = CHUNKS // QUAD
 QW = QUAD * P
 TW = P
 VW = QW - TW
+ROW_ORDER = (0, 3, 1, 4, 2, 5)
+TURN_AFTER = {3: (0,), 4: (1, 2), 5: (3, 4)}
 OFFSET = 12582912.0
 
 FLOPS = 2 * ROWS * D * COLS
@@ -54,6 +56,12 @@ def tile_ka_attention_heads_mod_pa_kernel(
         coef_sb = keep.tile([P, CHUNKS, P * PLANES], BF16)
         turns = keep.tile([P, PLANES], F32)
         bias_t = keep.tile([P, COL_BLOCKS], F32)
+
+        periods = whole.enter_context(tc.tile_pool(name="periods", bufs=2))
+        scaled = whole.enter_context(tc.tile_pool(name="scaled", bufs=3))
+        marks = whole.enter_context(tc.tile_pool(name="marks", bufs=2))
+        backs = whole.enter_context(tc.tile_pool(name="backs", bufs=2))
+        ps_frac = whole.enter_context(tc.psum_pool(name="ps_frac", bufs=2))
 
         with ExitStack() as first:
             stage = first.enter_context(tc.tile_pool(name="stage", bufs=1))
@@ -102,7 +110,7 @@ def tile_ka_attention_heads_mod_pa_kernel(
             nc.vector.tensor_copy(out=bias_t[:], in_=bt[:, 0:COL_BLOCKS])
 
             grouped_w = grouped[:].bitcast(F32).rearrange("p (r u) -> p r u", u=2)
-            for rt in range(ROW_TILES):
+            for rt in ROW_ORDER:
                 rows = slice(rt * P, (rt + 1) * P)
                 xt = ps_x.tile([P, 2, P], F32)
                 x_words = x_sb[:, rt, :].bitcast(F32)
@@ -111,15 +119,13 @@ def tile_ka_attention_heads_mod_pa_kernel(
                 nc.vector.tensor_copy(
                     out=grouped_w[:, rows, :], in_=xt[:].rearrange("p u r -> p r u")
                 )
-            for rt in range(ROW_TILES):
-                rows = slice(rt * P, (rt + 1) * P)
                 nc.vector.quantize_mx(
                     out=x_codes[:, rows].bitcast(FP8X4),
                     scales=x_scales[:, rows],
                     in_=grouped[:, rt * 4 * P : (rt + 1) * 4 * P],
                 )
 
-            for rt in range(ROW_TILES):
+            for rt in ROW_ORDER:
                 rows = slice(rt * P, (rt + 1) * P)
                 b, third = divmod(rt, ROW_TILES // B)
                 xl_rows = xl[:, b, :].rearrange("p (r c) -> p r c", c=COL_BLOCKS)
@@ -143,24 +149,19 @@ def tile_ka_attention_heads_mod_pa_kernel(
                         op=ALU.add,
                     )
 
-            for j in range(G):
-                for b in range(B):
-                    group = xl[:, b, j * CHUNKS * P : (j + 1) * CHUNKS * P]
-                    firsts = group.rearrange("p (s c) -> p s c", c=QW)[:, :, 0:TW]
-                    mm = ps_mm.tile([P, QUADS_M, TW], F32)
-                    for cq in range(QUADS_M):
-                        nc.tensor.transpose(mm[:, cq, :], firsts[:, cq, :], ident[:])
-                    nc.scalar.copy(out=firsts, in_=mm[:])
+                for j in TURN_AFTER.get(rt, ()):
+                    for bb in range(B):
+                        group = xl[:, bb, j * CHUNKS * P : (j + 1) * CHUNKS * P]
+                        firsts = group.rearrange("p (s c) -> p s c", c=QW)[:, :, 0:TW]
+                        mm = ps_mm.tile([P, QUADS_M, TW], F32)
+                        for cq in range(QUADS_M):
+                            nc.tensor.transpose(mm[:, cq, :], firsts[:, cq, :], ident[:])
+                        nc.scalar.copy(out=firsts, in_=mm[:])
 
-        periods = whole.enter_context(tc.tile_pool(name="periods", bufs=2))
-        scaled = whole.enter_context(tc.tile_pool(name="scaled", bufs=3))
-        marks = whole.enter_context(tc.tile_pool(name="marks", bufs=2))
-        backs = whole.enter_context(tc.tile_pool(name="backs", bufs=2))
         waves = whole.enter_context(tc.tile_pool(name="waves", bufs=3))
         shifts = whole.enter_context(tc.tile_pool(name="shifts", bufs=2))
         results = whole.enter_context(tc.tile_pool(name="results", bufs=3))
         ps_coef = whole.enter_context(tc.psum_pool(name="ps_coef", bufs=4))
-        ps_frac = whole.enter_context(tc.psum_pool(name="ps_frac", bufs=2))
         ps_sum = whole.enter_context(tc.psum_pool(name="ps_sum", bufs=1))
         ps_hold = whole.enter_context(tc.psum_pool(name="ps_hold", bufs=1))
 

@@ -268,8 +268,8 @@ def tile_ka_attention_heads_mod_pa_kernel(
         def subtract(v):
             k = k_of.pop(v)
             wave = waves.tile([P, B, 2, QW], F32)
-            for first, n, xq, turn in runs(v):
-                for h in range(n):
+            for first, n, xq, turn in reversed(runs(v)):
+                for h in reversed(range(n)):
                     nc.vector.scalar_tensor_tensor(
                         out=wave[:, :, first + h, TW:QW],
                         in0=xq[:, :, h, TW:QW],

@@ -33,11 +33,14 @@ QUADS_M = CHUNKS // QUAD
 QW = QUAD * P
 TW = P
 VW = QW - TW
-ROW_ORDER = (0, 3, 1, 4, 2, 5)
-TURN_AFTER = {3: (0,), 4: (1, 2), 5: (3, 4)}
+THIRDS = ROW_TILES // B
 OFFSET = 12582912.0
 
 FLOPS = 2 * ROWS * D * COLS
+
+
+def turned_batches(j):
+    return B if j % 2 == 0 else B - 1
 
 
 def tile_ka_attention_heads_mod_pa_kernel(
@@ -57,115 +60,22 @@ def tile_ka_attention_heads_mod_pa_kernel(
         turns = keep.tile([P, PLANES], F32)
         bias_t = keep.tile([P, COL_BLOCKS], F32)
 
+        x_sb = coef_sb[:, CHUNKS - 1, 0 : ROW_TILES * D].rearrange("p (t d) -> p t d", d=D)
+        grouped = coef_sb[:, CHUNKS - 2, 0 : ROWS * 4]
+        grouped_w = grouped.bitcast(F32).rearrange("p (r u) -> p r u", u=2)
+
         periods = whole.enter_context(tc.tile_pool(name="periods", bufs=2))
         scaled = whole.enter_context(tc.tile_pool(name="scaled", bufs=3))
         marks = whole.enter_context(tc.tile_pool(name="marks", bufs=2))
         backs = whole.enter_context(tc.tile_pool(name="backs", bufs=2))
-        ps_frac = whole.enter_context(tc.psum_pool(name="ps_frac", bufs=2))
-
-        with ExitStack() as first:
-            stage = first.enter_context(tc.tile_pool(name="stage", bufs=1))
-            ps_x = first.enter_context(tc.psum_pool(name="ps_x", bufs=2))
-            ps_b = first.enter_context(tc.psum_pool(name="ps_b", bufs=1))
-            ps_mm = first.enter_context(tc.psum_pool(name="ps_mm", bufs=3))
-
-            x_sb = stage.tile([P, ROW_TILES, D], BF16)
-            w_words = stage.tile([P, 2 * COLS], U8, align_bytes=64)
-            w_scales = stage.tile([P, COLS], U8, align_bytes=64)
-            b_rows = stage.tile([P, P], BF16)
-            g_raw = stage.tile([P, PLANES], BF16)
-            ident_bf = stage.tile([P, P], BF16)
-            grouped = stage.tile([P, ROWS * 4], BF16, align_bytes=64)
-            x_codes = stage.tile([P, ROWS], U32, align_bytes=64)
-            x_scales = stage.tile([P, ROWS], U8, align_bytes=64)
-
-            nc.vector.memset(w_scales[:].bitcast(I32), 0)
-            nc.vector.memset(b_rows[:], 0.0)
-            make_identity(nc, ident_bf[:])
-
-            nc.sync.dma_start(
-                out=x_sb[:],
-                in_=x.rearrange("b h p d -> (b h p) d").rearrange("(t r) d -> r t d", r=P),
-            )
-            for quadrant in range(4):
-                nc.sync.dma_start(
-                    out=w_scales[32 * quadrant : 32 * quadrant + 4, :].bitcast(I32),
-                    in_=lin_w_scales[0, 4 * quadrant : 4 * quadrant + 4, :].bitcast(I32),
-                )
-            nc.sync.dma_start(out=w_words[:].bitcast(I32), in_=lin_w_words[0].bitcast(I32))
-            nc.sync.dma_start(
-                out=b_rows[0:COL_BLOCKS, :], in_=lin_b.rearrange("(c i) -> c i", i=P)
-            )
-            nc.sync.dma_start(
-                out=g_raw[:], in_=grid.rearrange("j m -> (j m)").partition_broadcast(P)
-            )
-            for c in range(CHUNKS):
-                nc.sync.dma_start(out=coef_sb[:, c, :], in_=coef_v[:, c, :])
-
-            nc.vector.tensor_scalar(
-                out=turns[:], in0=g_raw[:], scalar1=1.0 / TWO_PI, scalar2=None, op0=ALU.mult
-            )
-            bt = ps_b.tile([P, P], BF16)
-            nc.tensor.transpose(bt[:], b_rows[:], ident_bf[:])
-            nc.vector.tensor_copy(out=bias_t[:], in_=bt[:, 0:COL_BLOCKS])
-
-            grouped_w = grouped[:].bitcast(F32).rearrange("p (r u) -> p r u", u=2)
-            for rt in ROW_ORDER:
-                rows = slice(rt * P, (rt + 1) * P)
-                xt = ps_x.tile([P, 2, P], F32)
-                x_words = x_sb[:, rt, :].bitcast(F32)
-                for u in range(2):
-                    nc.tensor.transpose(xt[:, u, :], x_words[:, u : D // 2 : 2], ident[:])
-                nc.vector.tensor_copy(
-                    out=grouped_w[:, rows, :], in_=xt[:].rearrange("p u r -> p r u")
-                )
-                nc.vector.quantize_mx(
-                    out=x_codes[:, rows].bitcast(FP8X4),
-                    scales=x_scales[:, rows],
-                    in_=grouped[:, rt * 4 * P : (rt + 1) * 4 * P],
-                )
-
-            for rt in ROW_ORDER:
-                rows = slice(rt * P, (rt + 1) * P)
-                b, third = divmod(rt, ROW_TILES // B)
-                xl_rows = xl[:, b, :].rearrange("p (r c) -> p r c", c=COL_BLOCKS)
-                for a in range(COL_BLOCKS // 4):
-                    mm = ps_mm.tile([P, 4, P], F32)
-                    for g in range(4):
-                        cb = 4 * a + g
-                        nc.tensor.matmul_mx(
-                            out=mm[:, g, :],
-                            lhsT=w_words[:, cb * 2 * P : (cb + 1) * 2 * P].bitcast(FP4X4),
-                            lhsT_scale=w_scales[:, cb * P : (cb + 1) * P],
-                            rhs=x_codes[:, rows].bitcast(FP8X4),
-                            rhs_scale=x_scales[:, rows],
-                            start=True,
-                            stop=True,
-                        )
-                    nc.vector.tensor_tensor(
-                        out=xl_rows[:, third * P : (third + 1) * P, 4 * a : 4 * a + 4],
-                        in0=mm[:].rearrange("p g r -> p r g"),
-                        in1=bias_t[:, 4 * a : 4 * a + 4].unsqueeze(1).to_broadcast([P, P, 4]),
-                        op=ALU.add,
-                    )
-
-                for j in TURN_AFTER.get(rt, ()):
-                    for bb in range(B):
-                        group = xl[:, bb, j * CHUNKS * P : (j + 1) * CHUNKS * P]
-                        firsts = group.rearrange("p (s c) -> p s c", c=QW)[:, :, 0:TW]
-                        mm = ps_mm.tile([P, QUADS_M, TW], F32)
-                        for cq in range(QUADS_M):
-                            nc.tensor.transpose(mm[:, cq, :], firsts[:, cq, :], ident[:])
-                        nc.scalar.copy(out=firsts, in_=mm[:])
-
-        waves = whole.enter_context(tc.tile_pool(name="waves", bufs=3))
+        waves = whole.enter_context(tc.tile_pool(name="waves", bufs=2))
         shifts = whole.enter_context(tc.tile_pool(name="shifts", bufs=2))
-        results = whole.enter_context(tc.tile_pool(name="results", bufs=3))
-        ps_coef = whole.enter_context(tc.psum_pool(name="ps_coef", bufs=4))
-        ps_sum = whole.enter_context(tc.psum_pool(name="ps_sum", bufs=1))
-        ps_hold = whole.enter_context(tc.psum_pool(name="ps_hold", bufs=1))
+        ps_frac = whole.enter_context(tc.psum_pool(name="ps_frac", bufs=2))
+        ps_coef = whole.enter_context(tc.psum_pool(name="ps_coef", bufs=3))
 
         n_planes = OUT_J * G
+        pools = {}
+        coef_banks = []
         k_of, t_of, mark_of, back_of, frac_of, coef_of, wave_of, total_of, shift_of, turned = (
             {}, {}, {}, {}, {}, {}, {}, {}, {}, {},
         )
@@ -207,15 +117,26 @@ def tile_ka_attention_heads_mod_pa_kernel(
 
         def scale_up(v):
             t = scaled.tile([P, B, 2, TW], F32)
+            nb = turned_batches(v % G)
             for first, n, xq, turn in runs(v):
                 nc.scalar.activation(
-                    out=t[:, :, first : first + n, :], in_=xq[:, :, :, 0:TW], func=ACT.Copy, scale=turn
+                    out=t[:, 0:nb, first : first + n, :],
+                    in_=xq[:, 0:nb, :, 0:TW],
+                    func=ACT.Copy,
+                    scale=turn,
                 )
             t_of[v] = t
 
         def round_off(v):
             mark = marks.tile([P, B, 2, TW], U32)
-            nc.scalar.activation(out=mark[:], in_=t_of[v][:], func=ACT.Copy, scale=1.0, bias=OFFSET)
+            for first, n, xq, turn in runs(v):
+                nc.scalar.activation(
+                    out=mark[:, :, first : first + n, :],
+                    in_=xq[:, :, :, 0:TW],
+                    func=ACT.Copy,
+                    scale=turn,
+                    bias=OFFSET,
+                )
             mark_of[v] = mark
 
         def negate(v):
@@ -226,9 +147,9 @@ def tile_ka_attention_heads_mod_pa_kernel(
             back_of[v] = back
 
         def take_off(v):
-            t, back = t_of.pop(v), back_of.pop(v)
+            t, back = t_of.pop(v), back_of[v]
             frac = ps_frac.tile([P, B, 2, TW], F32)
-            for b in range(B):
+            for b in range(turned_batches(v % G)):
                 for half in range(2):
                     for step, src in enumerate((t, back)):
                         nc.tensor.matmul(
@@ -241,16 +162,19 @@ def tile_ka_attention_heads_mod_pa_kernel(
                         )
             frac_of[v] = frac
 
-        def turn_coef(v):
+        def turn_coef(v, halves=(0, 1)):
             j = v % G
-            fresh = {}
-            coef_of[v] = []
-            for m, cq in quads(v):
+            for half in halves:
+                m, cq = quads(v)[half]
                 key = ((m * G + j) // 2, cq)
                 far = cq == 1 and m % 2 == 0 and j == G - 1
-                coef_t = held.pop(key) if key in held else turned.get(key)
+                coef_t = held.pop(key) if key in held else turned.pop(key, None)
                 if coef_t is None:
-                    pool = ps_hold if far else ps_coef
+                    if far:
+                        pool = pools["hold"]
+                    else:
+                        pool = pools["coef"] if len(coef_banks) % 4 == 3 else ps_coef
+                        coef_banks.append(key)
                     coef_t = pool.tile([P, QUAD, P], F32)
                     for cl in range(QUAD):
                         words = coef_sb[:, cq * QUAD + cl, :].bitcast(F32)
@@ -259,15 +183,26 @@ def tile_ka_attention_heads_mod_pa_kernel(
                         )
                     if far:
                         held[key] = coef_t
-                fresh[key] = coef_t
-                coef_of[v].append(coef_t)
-            turned.clear()
-            for key in fresh:
-                turned[key] = fresh[key]
+                    else:
+                        turned[key] = coef_t
+                coef_of[v, half] = coef_t
 
         def subtract(v):
             k = k_of.pop(v)
-            wave = waves.tile([P, B, 2, QW], F32)
+            pool = pools["waves"] if v % 3 == 2 else waves
+            wave = pool.tile([P, B, 2, QW], F32)
+            nb = turned_batches(v % G)
+            back = back_of.pop(v)
+            for first, n, xq, turn in runs(v):
+                for b in range(nb, B):
+                    nc.vector.scalar_tensor_tensor(
+                        out=wave[:, b, first : first + n, 0:TW],
+                        in0=xq[:, b, :, 0:TW],
+                        scalar=turn,
+                        in1=back[:, b, first : first + n, :],
+                        op0=ALU.mult,
+                        op1=ALU.add,
+                    )
             for first, n, xq, turn in reversed(runs(v)):
                 for h in reversed(range(n)):
                     nc.vector.scalar_tensor_tensor(
@@ -281,18 +216,25 @@ def tile_ka_attention_heads_mod_pa_kernel(
             wave_of[v] = wave
 
         def sine_tensor_way(v):
+            nb = turned_batches(v % G)
             nc.scalar.activation(
-                out=wave_of[v][:, :, :, 0:TW], in_=frac_of.pop(v)[:], func=ACT.Sin, scale=TWO_PI
+                out=wave_of[v][:, 0:nb, :, 0:TW],
+                in_=frac_of.pop(v)[:, 0:nb, :, :],
+                func=ACT.Sin,
+                scale=TWO_PI,
             )
 
         def sine_vector_way(v):
-            rest = wave_of[v][:, :, :, TW:QW]
-            nc.scalar.activation(out=rest, in_=rest, func=ACT.Sin, scale=TWO_PI)
+            nb = turned_batches(v % G)
+            pieces = [wave_of[v][:, :, :, TW:QW]]
+            pieces += [wave_of[v][:, b, :, 0:TW] for b in range(nb, B)]
+            for piece in pieces:
+                nc.scalar.activation(out=piece, in_=piece, func=ACT.Sin, scale=TWO_PI)
 
         def weigh(v, half):
             j = v % G
             m, cq = quads(v)[half]
-            pairs = coef_of[v][half][:].bitcast(BF16).rearrange("p c (q h) -> p c q h", h=2)
+            pairs = coef_of.pop((v, half))[:].bitcast(BF16).rearrange("p c (q h) -> p c q h", h=2)
             part = wave_of[v][:, :, half, :].rearrange("p b (c q) -> p b c q", c=QUAD)
             nc.vector.tensor_tensor(
                 out=part,
@@ -303,8 +245,7 @@ def tile_ka_attention_heads_mod_pa_kernel(
 
         def add_up(v):
             wave = wave_of.pop(v)
-            coef_of.pop(v)
-            total = ps_sum.tile([P, B, P], F32)
+            total = pools["sum"].tile([P, B, P], F32)
             for b in range(B):
                 for t in range(2 * QUAD):
                     half, cl = divmod(t, QUAD)
@@ -325,7 +266,7 @@ def tile_ka_attention_heads_mod_pa_kernel(
 
         def finish(v):
             o, j = divmod(v, G)
-            res = results.tile([P, B, P], F32)
+            res = pools["results"].tile([P, B, P], F32)
             nc.vector.tensor_tensor(
                 out=res[:],
                 in0=total_of.pop(v)[:],
@@ -334,50 +275,209 @@ def tile_ka_attention_heads_mod_pa_kernel(
             )
             nc.sync.dma_start(out=out_v[:, :, j * OUT_J + o, :], in_=res[:])
 
-        with tc.manual_schedule():
+
+        whole.enter_context(tc.manual_schedule())
+        with ExitStack() as first:
+            stage = first.enter_context(tc.tile_pool(name="stage", bufs=1))
+            ps_mm = first.enter_context(tc.psum_pool(name="ps_mm", bufs=3))
+
+            w_words = stage.tile([P, 2 * COLS], U8, align_bytes=64)
+            w_scales = stage.tile([P, COLS], U8, align_bytes=64)
+            b_rows = stage.tile([P, P], BF16)
+            g_raw = stage.tile([P, PLANES], BF16)
+            ident_bf = stage.tile([P, P], BF16)
+            x_codes = stage.tile([P, ROWS], U32, align_bytes=64)
+            x_scales = stage.tile([P, ROWS], U8, align_bytes=64)
+
+            x_rows = x.rearrange("b h p d -> (b h p) d").rearrange(
+                "(b t r) d -> r b t d", r=P, b=B
+            )
+            x_tiles = x_sb.rearrange("p (b t) d -> p b t d", b=B)
+
+            def load_x(third):
+                nc.sync.dma_start(out=x_tiles[:, :, third, :], in_=x_rows[:, :, third, :])
+
+            def load_coef(c):
+                nc.sync.dma_start(out=coef_sb[:, c, :], in_=coef_v[:, c, :])
+
+            def group_x(rt):
+                rows = slice(rt * P, (rt + 1) * P)
+                mm = ps_mm.tile([P, 4, P], F32)
+                x_words = x_sb[:, rt, :].bitcast(F32)
+                for u in range(2):
+                    nc.tensor.transpose(mm[:, u, :], x_words[:, u : D // 2 : 2], ident[:])
+                nc.scalar.copy(out=grouped_w[:, rows, :], in_=mm[:, 0:2, :].rearrange("p u r -> p r u"))
+
+            def quantize(rt):
+                rows = slice(rt * P, (rt + 1) * P)
+                nc.vector.quantize_mx(
+                    out=x_codes[:, rows].bitcast(FP8X4),
+                    scales=x_scales[:, rows],
+                    in_=grouped[:, rt * 4 * P : (rt + 1) * 4 * P],
+                )
+
+            def project(rt, a):
+                rows = slice(rt * P, (rt + 1) * P)
+                b, third = divmod(rt, THIRDS)
+                xl_rows = xl[:, b, :].rearrange("p (r c) -> p r c", c=COL_BLOCKS)
+                mm = ps_mm.tile([P, 4, P], F32)
+                for g in range(4):
+                    cb = 4 * a + g
+                    nc.tensor.matmul_mx(
+                        out=mm[:, g, :],
+                        lhsT=w_words[:, cb * 2 * P : (cb + 1) * 2 * P].bitcast(FP4X4),
+                        lhsT_scale=w_scales[:, cb * P : (cb + 1) * P],
+                        rhs=x_codes[:, rows].bitcast(FP8X4),
+                        rhs_scale=x_scales[:, rows],
+                        start=True,
+                        stop=True,
+                    )
+                nc.vector.tensor_tensor(
+                    out=xl_rows[:, third * P : (third + 1) * P, 4 * a : 4 * a + 4],
+                    in0=mm[:].rearrange("p g r -> p r g"),
+                    in1=bias_t[:, 4 * a : 4 * a + 4].unsqueeze(1).to_broadcast([P, P, 4]),
+                    op=ALU.add,
+                )
+
+            def turn(j):
+                for bb in range(turned_batches(j)):
+                    group = xl[:, bb, j * CHUNKS * P : (j + 1) * CHUNKS * P]
+                    firsts = group.rearrange("p (s c) -> p s c", c=QW)[:, :, 0:TW]
+                    mm = ps_mm.tile([P, 4, P], F32)
+                    for cq in range(QUADS_M):
+                        nc.tensor.transpose(mm[:, cq, :], firsts[:, cq, :], ident[:])
+                    nc.scalar.copy(out=firsts, in_=mm[:, 0:QUADS_M, :])
+
+            load_x(0)
+            nc.vector.memset(w_scales[:].bitcast(I32), 0)
+            nc.vector.memset(b_rows[:], 0.0)
+            for quadrant in range(4):
+                nc.sync.dma_start(
+                    out=w_scales[32 * quadrant : 32 * quadrant + 4, :].bitcast(I32),
+                    in_=lin_w_scales[0, 4 * quadrant : 4 * quadrant + 4, :].bitcast(I32),
+                )
+            nc.sync.dma_start(out=w_words[:].bitcast(I32), in_=lin_w_words[0].bitcast(I32))
+            nc.sync.dma_start(
+                out=b_rows[0:COL_BLOCKS, :], in_=lin_b.rearrange("(c i) -> c i", i=P)
+            )
+            nc.sync.dma_start(
+                out=g_raw[:], in_=grid.rearrange("j m -> (j m)").partition_broadcast(P)
+            )
+            load_x(1)
+            load_x(2)
+            for c in range(2 * QUAD):
+                load_coef(c)
             load_shift(0)
+            for c in range(2 * QUAD, CHUNKS - 2):
+                load_coef(c)
+            make_identity(nc, ident_bf[:])
+
+            blocks = range(COL_BLOCKS // 4)
+            for rt in (0, THIRDS):
+                group_x(rt)
+                quantize(rt)
+            nc.vector.tensor_scalar(
+                out=turns[:], in0=g_raw[:], scalar1=1.0 / TWO_PI, scalar2=None, op0=ALU.mult
+            )
+            mm = ps_mm.tile([P, 8, P], BF16)
+            nc.tensor.transpose(mm[:, 0, :], b_rows[:], ident_bf[:])
+            nc.vector.tensor_copy(out=bias_t[:], in_=mm[:, 0, 0:COL_BLOCKS])
+            for a in blocks:
+                project(0, a)
+            for rt in (1, THIRDS + 1):
+                group_x(rt)
+                quantize(rt)
+            for a in blocks:
+                project(THIRDS, a)
+            for a in blocks[:2]:
+                project(1, a)
+            turn(0)
             count_periods(0)
             count_periods(1)
             scale_up(0)
-            scale_up(1)
             round_off(0)
+            for a in blocks[2:]:
+                project(1, a)
+            for rt in (2, THIRDS + 2):
+                group_x(rt)
+                quantize(rt)
+            for c in range(CHUNKS - 2, CHUNKS):
+                load_coef(c)
             negate(0)
-            round_off(1)
-            negate(1)
-            scale_up(2)
+            for a in blocks[:2]:
+                project(THIRDS + 1, a)
             take_off(0)
+            for a in blocks[2:]:
+                project(THIRDS + 1, a)
             subtract(0)
             sine_tensor_way(0)
-            round_off(2)
             sine_vector_way(0)
-            turn_coef(0)
-            take_off(1)
+            for a in blocks[:2]:
+                project(2, a)
+            turn(1)
+            scale_up(1)
+            round_off(1)
+            turn_coef(0, (0,))
+            for a in blocks[2:]:
+                project(2, a)
+            turn(2)
+            negate(1)
+            scale_up(2)
+            round_off(2)
+            weigh(0, 0)
             count_periods(2)
-            scale_up(3)
-            for v in range(n_planes):
-                if v % G == 0 and v // G + 1 < OUT_J:
-                    load_shift(v // G + 1)
-                if v >= 1:
-                    add_up(v - 1)
-                if v + 2 < n_planes:
-                    negate(v + 2)
-                if v + 3 < n_planes:
-                    round_off(v + 3)
-                if v + 4 < n_planes:
-                    scale_up(v + 4)
-                if v + 1 < n_planes:
-                    subtract(v + 1)
-                if v + 3 < n_planes:
-                    count_periods(v + 3)
-                if v + 1 < n_planes:
-                    sine_tensor_way(v + 1)
-                    turn_coef(v + 1)
-                    sine_vector_way(v + 1)
+            for a in blocks[:3]:
+                project(THIRDS + 2, a)
+            take_off(1)
+            for a in blocks[3:]:
+                project(THIRDS + 2, a)
+            subtract(1)
+            negate(2)
+            sine_tensor_way(1)
+            turn(3)
+            sine_vector_way(1)
+            turn(4)
+
+        pools["waves"] = whole.enter_context(tc.tile_pool(name="late_waves", bufs=1))
+        pools["results"] = whole.enter_context(tc.tile_pool(name="results", bufs=3))
+        pools["coef"] = whole.enter_context(tc.psum_pool(name="ps_late_coef", bufs=1))
+        pools["sum"] = whole.enter_context(tc.psum_pool(name="ps_sum", bufs=1))
+        pools["hold"] = whole.enter_context(tc.psum_pool(name="ps_hold", bufs=1))
+
+        turn_coef(0, (1,))
+        weigh(0, 1)
+        turn_coef(1, (0,))
+        weigh(1, 0)
+        scale_up(3)
+        round_off(3)
+        scale_up(4)
+        take_off(2)
+        count_periods(3)
+        turn_coef(1, (1,))
+        load_shift(1)
+        for v in range(1, n_planes):
+            if v % G == 0 and v // G + 1 < OUT_J:
+                load_shift(v // G + 1)
+            add_up(v - 1)
+            if v + 2 < n_planes:
+                negate(v + 2)
+            if v + 3 < n_planes:
+                round_off(v + 3)
+            if v + 4 < n_planes:
+                scale_up(v + 4)
+            if v + 1 < n_planes:
+                subtract(v + 1)
+            if v + 3 < n_planes:
+                count_periods(v + 3)
+            if v + 1 < n_planes:
+                sine_tensor_way(v + 1)
+                turn_coef(v + 1)
+                sine_vector_way(v + 1)
+            if v >= 2:
                 weigh(v, 0)
-                if v >= 1:
-                    finish(v - 1)
-                weigh(v, 1)
-                if v + 2 < n_planes:
-                    take_off(v + 2)
-            add_up(n_planes - 1)
-            finish(n_planes - 1)
+            finish(v - 1)
+            weigh(v, 1)
+            if v + 2 < n_planes:
+                take_off(v + 2)
+        add_up(n_planes - 1)
+        finish(n_planes - 1)

@@ -21,7 +21,7 @@ ROWS_B = H * POS
 ROW_TILES = ROWS // P
 COLS = G * D
 COL_BLOCKS = COLS // P
-BLOCKS_B = ROWS_B * COL_BLOCKS
+THIRD = P * COL_BLOCKS
 CHUNKS = 12
 QUAD = 4
 QUADS_J = NF * CHUNKS // QUAD
@@ -31,16 +31,14 @@ WORDS = PLANES // 2
 TWO_PI = 2.0 * math.pi
 QUADS_M = CHUNKS // QUAD
 QW = QUAD * P
+QUADS_T = THIRD // QW
 TW = P
 VW = QW - TW
+WARM = 512
 THIRDS = ROW_TILES // B
 OFFSET = 12582912.0
 
 FLOPS = 2 * ROWS * D * COLS
-
-
-def turned_batches(j):
-    return B if j % 2 == 0 else B - 1
 
 
 def tile_ka_attention_heads_mod_pa_kernel(
@@ -55,13 +53,17 @@ def tile_ka_attention_heads_mod_pa_kernel(
         keep = whole.enter_context(tc.tile_pool(name="keep", bufs=1))
         ident = keep.tile([P, P], F32)
         make_identity(nc, ident[:])
-        xl = keep.tile([P, B, BLOCKS_B], F32)
-        coef_sb = keep.tile([P, CHUNKS, P * PLANES], BF16)
+        xl = [keep.tile([P, B, THIRD], F32, name=f"xl{third}") for third in range(THIRDS)]
+        coef_sb = [keep.tile([P, P * PLANES], BF16, name=f"coef{c}") for c in range(CHUNKS)]
         turns = keep.tile([P, PLANES], F32)
         bias_t = keep.tile([P, COL_BLOCKS], F32)
+        codes_a = keep.tile([P, WARM], U32, align_bytes=64)
+        scales_a = keep.tile([P, WARM], U8, align_bytes=64)
+        warm_words = keep.tile([P, 2 * P], U8, align_bytes=64)
+        warm_scales = keep.tile([P, P], U8, align_bytes=64)
 
-        x_sb = coef_sb[:, CHUNKS - 1, 0 : ROW_TILES * D].rearrange("p (t d) -> p t d", d=D)
-        grouped = coef_sb[:, CHUNKS - 2, 0 : ROWS * 4]
+        x_sb = coef_sb[CHUNKS - 1][:, 0 : ROW_TILES * D].rearrange("p (t b d) -> p t b d", b=B, d=D)
+        grouped = coef_sb[CHUNKS - 2][:, 0 : ROWS * 4]
         grouped_w = grouped.bitcast(F32).rearrange("p (r u) -> p r u", u=2)
 
         periods = whole.enter_context(tc.tile_pool(name="periods", bufs=2))
@@ -88,15 +90,19 @@ def tile_ka_attention_heads_mod_pa_kernel(
         def runs(v):
             j = v % G
             (m0, cq0), (m1, cq1) = quads(v)
-            pieces = [(0, 2, m0, cq0)] if m0 == m1 else [(0, 1, m0, cq0), (1, 1, m1, cq1)]
+            third0, third1 = ((j * QUADS_M + cq) // QUADS_T for cq in (cq0, cq1))
+            pieces = [(0, 2, m0, cq0)]
+            if m0 != m1 or third0 != third1:
+                pieces = [(0, 1, m0, cq0), (1, 1, m1, cq1)]
             found = []
             for first, n, m, cq in pieces:
-                y0 = (j * CHUNKS + cq * QUAD) * P
+                third, quad = divmod(j * QUADS_M + cq, QUADS_T)
+                x_run = xl[third][:, :, quad * QW : (quad + n) * QW]
                 found.append(
                     (
                         first,
                         n,
-                        xl[:, :, y0 : y0 + n * QW].rearrange("p b (h c) -> p b h c", c=QW),
+                        x_run.rearrange("p b (h c) -> p b h c", c=QW),
                         turns[:, j * NF + m : j * NF + m + 1],
                     )
                 )
@@ -117,11 +123,10 @@ def tile_ka_attention_heads_mod_pa_kernel(
 
         def scale_up(v):
             t = scaled.tile([P, B, 2, TW], F32)
-            nb = turned_batches(v % G)
             for first, n, xq, turn in runs(v):
                 nc.scalar.activation(
-                    out=t[:, 0:nb, first : first + n, :],
-                    in_=xq[:, 0:nb, :, 0:TW],
+                    out=t[:, :, first : first + n, :],
+                    in_=xq[:, :, :, 0:TW],
                     func=ACT.Copy,
                     scale=turn,
                 )
@@ -146,10 +151,24 @@ def tile_ka_attention_heads_mod_pa_kernel(
             )
             back_of[v] = back
 
+        def keep_clock(bank, passes):
+            for i in range(passes):
+                nc.tensor.matmul_mx(
+                    out=bank,
+                    lhsT=warm_words[:].bitcast(FP4X4),
+                    lhsT_scale=warm_scales[:],
+                    rhs=codes_a[:].bitcast(FP8X4),
+                    rhs_scale=scales_a[:],
+                    start=True,
+                    stop=True,
+                )
+
         def take_off(v):
-            t, back = t_of.pop(v), back_of[v]
+            t, back = t_of.pop(v), back_of.pop(v)
             frac = ps_frac.tile([P, B, 2, TW], F32)
-            for b in range(turned_batches(v % G)):
+            if v >= 2:
+                keep_clock(frac[:].rearrange("p b h c -> p (b h c)"), 1)
+            for b in range(B):
                 for half in range(2):
                     for step, src in enumerate((t, back)):
                         nc.tensor.matmul(
@@ -177,7 +196,7 @@ def tile_ka_attention_heads_mod_pa_kernel(
                         coef_banks.append(key)
                     coef_t = pool.tile([P, QUAD, P], F32)
                     for cl in range(QUAD):
-                        words = coef_sb[:, cq * QUAD + cl, :].bitcast(F32)
+                        words = coef_sb[cq * QUAD + cl][:].bitcast(F32)
                         nc.tensor.transpose(
                             coef_t[:, cl, :], words[:, key[0] : P * WORDS : WORDS], ident[:]
                         )
@@ -191,18 +210,6 @@ def tile_ka_attention_heads_mod_pa_kernel(
             k = k_of.pop(v)
             pool = pools["waves"] if v % 3 == 2 else waves
             wave = pool.tile([P, B, 2, QW], F32)
-            nb = turned_batches(v % G)
-            back = back_of.pop(v)
-            for first, n, xq, turn in runs(v):
-                for b in range(nb, B):
-                    nc.vector.scalar_tensor_tensor(
-                        out=wave[:, b, first : first + n, 0:TW],
-                        in0=xq[:, b, :, 0:TW],
-                        scalar=turn,
-                        in1=back[:, b, first : first + n, :],
-                        op0=ALU.mult,
-                        op1=ALU.add,
-                    )
             for first, n, xq, turn in reversed(runs(v)):
                 for h in reversed(range(n)):
                     nc.vector.scalar_tensor_tensor(
@@ -216,20 +223,13 @@ def tile_ka_attention_heads_mod_pa_kernel(
             wave_of[v] = wave
 
         def sine_tensor_way(v):
-            nb = turned_batches(v % G)
             nc.scalar.activation(
-                out=wave_of[v][:, 0:nb, :, 0:TW],
-                in_=frac_of.pop(v)[:, 0:nb, :, :],
-                func=ACT.Sin,
-                scale=TWO_PI,
+                out=wave_of[v][:, :, :, 0:TW], in_=frac_of.pop(v)[:], func=ACT.Sin, scale=TWO_PI
             )
 
         def sine_vector_way(v):
-            nb = turned_batches(v % G)
-            pieces = [wave_of[v][:, :, :, TW:QW]]
-            pieces += [wave_of[v][:, b, :, 0:TW] for b in range(nb, B)]
-            for piece in pieces:
-                nc.scalar.activation(out=piece, in_=piece, func=ACT.Sin, scale=TWO_PI)
+            rest = wave_of[v][:, :, :, TW:QW]
+            nc.scalar.activation(out=rest, in_=rest, func=ACT.Sin, scale=TWO_PI)
 
         def weigh(v, half):
             j = v % G
@@ -245,7 +245,9 @@ def tile_ka_attention_heads_mod_pa_kernel(
 
         def add_up(v):
             wave = wave_of.pop(v)
-            total = pools["sum"].tile([P, B, P], F32)
+            bank = pools["sum"].tile([P, WARM], F32)
+            keep_clock(bank[:], 3 if v % G == 0 else 1)
+            total = bank[:, 0 : B * P].rearrange("p (b q) -> p b q", b=B)
             for b in range(B):
                 for t in range(2 * QUAD):
                     half, cl = divmod(t, QUAD)
@@ -269,7 +271,7 @@ def tile_ka_attention_heads_mod_pa_kernel(
             res = pools["results"].tile([P, B, P], F32)
             nc.vector.tensor_tensor(
                 out=res[:],
-                in0=total_of.pop(v)[:],
+                in0=total_of.pop(v),
                 in1=shift_of[o][:, j, :].unsqueeze(1).to_broadcast([P, B, P]),
                 op=ALU.add,
             )
@@ -286,40 +288,46 @@ def tile_ka_attention_heads_mod_pa_kernel(
             b_rows = stage.tile([P, P], BF16)
             g_raw = stage.tile([P, PLANES], BF16)
             ident_bf = stage.tile([P, P], BF16)
-            x_codes = stage.tile([P, ROWS], U32, align_bytes=64)
-            x_scales = stage.tile([P, ROWS], U8, align_bytes=64)
+            codes_b = stage.tile([P, ROWS - WARM], U32, align_bytes=64)
+            scales_b = stage.tile([P, ROWS - WARM], U8, align_bytes=64)
+
+            def x_codes(rt):
+                codes, scales, at = codes_a, scales_a, rt * P
+                if at >= WARM:
+                    codes, scales, at = codes_b, scales_b, at - WARM
+                return codes[:, at : at + P].bitcast(FP8X4), scales[:, at : at + P]
 
             x_rows = x.rearrange("b h p d -> (b h p) d").rearrange(
-                "(b t r) d -> r b t d", r=P, b=B
+                "(b t r) d -> r t b d", r=P, b=B
             )
-            x_tiles = x_sb.rearrange("p (b t) d -> p b t d", b=B)
 
             def load_x(third):
-                nc.sync.dma_start(out=x_tiles[:, :, third, :], in_=x_rows[:, :, third, :])
+                nc.sync.dma_start(out=x_sb[:, third, :, :], in_=x_rows[:, third, :, :])
 
             def load_coef(c):
-                nc.sync.dma_start(out=coef_sb[:, c, :], in_=coef_v[:, c, :])
+                nc.sync.dma_start(out=coef_sb[c][:], in_=coef_v[:, c, :])
 
             def group_x(rt):
                 rows = slice(rt * P, (rt + 1) * P)
+                b, third = divmod(rt, THIRDS)
                 mm = ps_mm.tile([P, 4, P], F32)
-                x_words = x_sb[:, rt, :].bitcast(F32)
+                x_words = x_sb[:, third, b, :].bitcast(F32)
                 for u in range(2):
                     nc.tensor.transpose(mm[:, u, :], x_words[:, u : D // 2 : 2], ident[:])
                 nc.scalar.copy(out=grouped_w[:, rows, :], in_=mm[:, 0:2, :].rearrange("p u r -> p r u"))
 
             def quantize(rt):
-                rows = slice(rt * P, (rt + 1) * P)
+                codes, scales = x_codes(rt)
                 nc.vector.quantize_mx(
-                    out=x_codes[:, rows].bitcast(FP8X4),
-                    scales=x_scales[:, rows],
+                    out=codes,
+                    scales=scales,
                     in_=grouped[:, rt * 4 * P : (rt + 1) * 4 * P],
                 )
 
             def project(rt, a):
-                rows = slice(rt * P, (rt + 1) * P)
+                codes, scales = x_codes(rt)
                 b, third = divmod(rt, THIRDS)
-                xl_rows = xl[:, b, :].rearrange("p (r c) -> p r c", c=COL_BLOCKS)
+                xl_rows = xl[third][:, b, :].rearrange("p (r c) -> p r c", c=COL_BLOCKS)
                 mm = ps_mm.tile([P, 4, P], F32)
                 for g in range(4):
                     cb = 4 * a + g
@@ -327,30 +335,33 @@ def tile_ka_attention_heads_mod_pa_kernel(
                         out=mm[:, g, :],
                         lhsT=w_words[:, cb * 2 * P : (cb + 1) * 2 * P].bitcast(FP4X4),
                         lhsT_scale=w_scales[:, cb * P : (cb + 1) * P],
-                        rhs=x_codes[:, rows].bitcast(FP8X4),
-                        rhs_scale=x_scales[:, rows],
+                        rhs=codes,
+                        rhs_scale=scales,
                         start=True,
                         stop=True,
                     )
                 nc.vector.tensor_tensor(
-                    out=xl_rows[:, third * P : (third + 1) * P, 4 * a : 4 * a + 4],
+                    out=xl_rows[:, :, 4 * a : 4 * a + 4],
                     in0=mm[:].rearrange("p g r -> p r g"),
                     in1=bias_t[:, 4 * a : 4 * a + 4].unsqueeze(1).to_broadcast([P, P, 4]),
                     op=ALU.add,
                 )
 
-            def turn(j):
-                for bb in range(turned_batches(j)):
-                    group = xl[:, bb, j * CHUNKS * P : (j + 1) * CHUNKS * P]
-                    firsts = group.rearrange("p (s c) -> p s c", c=QW)[:, :, 0:TW]
+            def turn(j, third):
+                lo = max(j * QUADS_M, third * QUADS_T)
+                hi = min((j + 1) * QUADS_M, (third + 1) * QUADS_T)
+                for bb in range(B):
+                    quads_t = xl[third][:, bb, :].rearrange("p (s c) -> p s c", c=QW)
+                    firsts = quads_t[:, lo - third * QUADS_T : hi - third * QUADS_T, 0:TW]
                     mm = ps_mm.tile([P, 4, P], F32)
-                    for cq in range(QUADS_M):
-                        nc.tensor.transpose(mm[:, cq, :], firsts[:, cq, :], ident[:])
-                    nc.scalar.copy(out=firsts, in_=mm[:, 0:QUADS_M, :])
+                    for s in range(hi - lo):
+                        nc.tensor.transpose(mm[:, s, :], firsts[:, s, :], ident[:])
+                    nc.scalar.copy(out=firsts, in_=mm[:, 0 : hi - lo, :])
 
             load_x(0)
             nc.vector.memset(w_scales[:].bitcast(I32), 0)
             nc.vector.memset(b_rows[:], 0.0)
+            nc.vector.memset(warm_scales[:].bitcast(I32), 0)
             for quadrant in range(4):
                 nc.sync.dma_start(
                     out=w_scales[32 * quadrant : 32 * quadrant + 4, :].bitcast(I32),
@@ -368,6 +379,14 @@ def tile_ka_attention_heads_mod_pa_kernel(
             for c in range(2 * QUAD):
                 load_coef(c)
             load_shift(0)
+            for quadrant in range(4):
+                nc.sync.dma_start(
+                    out=warm_scales[32 * quadrant : 32 * quadrant + 4, :].bitcast(I32),
+                    in_=lin_w_scales[0, 4 * quadrant : 4 * quadrant + 4, 0:P].bitcast(I32),
+                )
+            nc.sync.dma_start(
+                out=warm_words[:].bitcast(I32), in_=lin_w_words[0][:, 0 : 2 * P].bitcast(I32)
+            )
             for c in range(2 * QUAD, CHUNKS - 2):
                 load_coef(c)
             make_identity(nc, ident_bf[:])
@@ -391,7 +410,8 @@ def tile_ka_attention_heads_mod_pa_kernel(
                 project(THIRDS, a)
             for a in blocks[:2]:
                 project(1, a)
-            turn(0)
+            turn(0, 0)
+            turn(1, 0)
             count_periods(0)
             count_periods(1)
             scale_up(0)
@@ -414,13 +434,14 @@ def tile_ka_attention_heads_mod_pa_kernel(
             sine_vector_way(0)
             for a in blocks[:2]:
                 project(2, a)
-            turn(1)
+            turn(1, 1)
             scale_up(1)
             round_off(1)
             turn_coef(0, (0,))
             for a in blocks[2:]:
                 project(2, a)
-            turn(2)
+            turn(2, 1)
+            turn(3, 1)
             negate(1)
             scale_up(2)
             round_off(2)
@@ -434,9 +455,9 @@ def tile_ka_attention_heads_mod_pa_kernel(
             subtract(1)
             negate(2)
             sine_tensor_way(1)
-            turn(3)
+            turn(3, 2)
             sine_vector_way(1)
-            turn(4)
+            turn(4, 2)
 
         pools["waves"] = whole.enter_context(tc.tile_pool(name="late_waves", bufs=1))
         pools["results"] = whole.enter_context(tc.tile_pool(name="results", bufs=3))
@@ -445,17 +466,28 @@ def tile_ka_attention_heads_mod_pa_kernel(
         pools["hold"] = whole.enter_context(tc.psum_pool(name="ps_hold", bufs=1))
 
         turn_coef(0, (1,))
-        weigh(0, 1)
-        turn_coef(1, (0,))
-        weigh(1, 0)
-        scale_up(3)
-        round_off(3)
-        scale_up(4)
         take_off(2)
+        weigh(0, 1)
+        subtract(2)
+        sine_tensor_way(2)
+        sine_vector_way(2)
+        turn_coef(1)
+        weigh(1, 0)
+        add_up(0)
         count_periods(3)
-        turn_coef(1, (1,))
+        round_off(3)
+        scale_up(3)
+        negate(3)
+        scale_up(4)
+        round_off(4)
+        scale_up(5)
+        take_off(3)
+        turn_coef(2)
+        finish(0)
+        weigh(1, 1)
         load_shift(1)
-        for v in range(1, n_planes):
+        count_periods(4)
+        for v in range(2, n_planes):
             if v % G == 0 and v // G + 1 < OUT_J:
                 load_shift(v // G + 1)
             add_up(v - 1)
@@ -473,8 +505,7 @@ def tile_ka_attention_heads_mod_pa_kernel(
                 sine_tensor_way(v + 1)
                 turn_coef(v + 1)
                 sine_vector_way(v + 1)
-            if v >= 2:
-                weigh(v, 0)
+            weigh(v, 0)
             finish(v - 1)
             weigh(v, 1)
             if v + 2 < n_planes:

@@ -34,11 +34,14 @@ QW = QUAD * P
 QUADS_T = THIRD // QW
 TW = P
 VW = QW - TW
-WARM = 512
 THIRDS = ROW_TILES // B
 OFFSET = 12582912.0
 
 FLOPS = 2 * ROWS * D * COLS
+
+
+def turned_batches(j):
+    return B if j % 2 == 0 else B - 1
 
 
 def tile_ka_attention_heads_mod_pa_kernel(
@@ -57,10 +60,6 @@ def tile_ka_attention_heads_mod_pa_kernel(
         coef_sb = [keep.tile([P, P * PLANES], BF16, name=f"coef{c}") for c in range(CHUNKS)]
         turns = keep.tile([P, PLANES], F32)
         bias_t = keep.tile([P, COL_BLOCKS], F32)
-        codes_a = keep.tile([P, WARM], U32, align_bytes=64)
-        scales_a = keep.tile([P, WARM], U8, align_bytes=64)
-        warm_words = keep.tile([P, 2 * P], U8, align_bytes=64)
-        warm_scales = keep.tile([P, P], U8, align_bytes=64)
 
         x_sb = coef_sb[CHUNKS - 1][:, 0 : ROW_TILES * D].rearrange("p (t b d) -> p t b d", b=B, d=D)
         grouped = coef_sb[CHUNKS - 2][:, 0 : ROWS * 4]
@@ -123,10 +122,11 @@ def tile_ka_attention_heads_mod_pa_kernel(
 
         def scale_up(v):
             t = scaled.tile([P, B, 2, TW], F32)
+            nb = turned_batches(v % G)
             for first, n, xq, turn in runs(v):
                 nc.scalar.activation(
-                    out=t[:, :, first : first + n, :],
-                    in_=xq[:, :, :, 0:TW],
+                    out=t[:, 0:nb, first : first + n, :],
+                    in_=xq[:, 0:nb, :, 0:TW],
                     func=ACT.Copy,
                     scale=turn,
                 )
@@ -151,24 +151,10 @@ def tile_ka_attention_heads_mod_pa_kernel(
             )
             back_of[v] = back
 
-        def keep_clock(bank, passes):
-            for i in range(passes):
-                nc.tensor.matmul_mx(
-                    out=bank,
-                    lhsT=warm_words[:].bitcast(FP4X4),
-                    lhsT_scale=warm_scales[:],
-                    rhs=codes_a[:].bitcast(FP8X4),
-                    rhs_scale=scales_a[:],
-                    start=True,
-                    stop=True,
-                )
-
         def take_off(v):
-            t, back = t_of.pop(v), back_of.pop(v)
+            t, back = t_of.pop(v), back_of[v]
             frac = ps_frac.tile([P, B, 2, TW], F32)
-            if v >= 2:
-                keep_clock(frac[:].rearrange("p b h c -> p (b h c)"), 1)
-            for b in range(B):
+            for b in range(turned_batches(v % G)):
                 for half in range(2):
                     for step, src in enumerate((t, back)):
                         nc.tensor.matmul(
@@ -210,6 +196,18 @@ def tile_ka_attention_heads_mod_pa_kernel(
             k = k_of.pop(v)
             pool = pools["waves"] if v % 3 == 2 else waves
             wave = pool.tile([P, B, 2, QW], F32)
+            nb = turned_batches(v % G)
+            back = back_of.pop(v)
+            for first, n, xq, turn in runs(v):
+                for b in range(nb, B):
+                    nc.vector.scalar_tensor_tensor(
+                        out=wave[:, b, first : first + n, 0:TW],
+                        in0=xq[:, b, :, 0:TW],
+                        scalar=turn,
+                        in1=back[:, b, first : first + n, :],
+                        op0=ALU.mult,
+                        op1=ALU.add,
+                    )
             for first, n, xq, turn in reversed(runs(v)):
                 for h in reversed(range(n)):
                     nc.vector.scalar_tensor_tensor(
@@ -223,13 +221,20 @@ def tile_ka_attention_heads_mod_pa_kernel(
             wave_of[v] = wave
 
         def sine_tensor_way(v):
+            nb = turned_batches(v % G)
             nc.scalar.activation(
-                out=wave_of[v][:, :, :, 0:TW], in_=frac_of.pop(v)[:], func=ACT.Sin, scale=TWO_PI
+                out=wave_of[v][:, 0:nb, :, 0:TW],
+                in_=frac_of.pop(v)[:, 0:nb, :, :],
+                func=ACT.Sin,
+                scale=TWO_PI,
             )
 
         def sine_vector_way(v):
-            rest = wave_of[v][:, :, :, TW:QW]
-            nc.scalar.activation(out=rest, in_=rest, func=ACT.Sin, scale=TWO_PI)
+            nb = turned_batches(v % G)
+            pieces = [wave_of[v][:, :, :, TW:QW]]
+            pieces += [wave_of[v][:, b, :, 0:TW] for b in range(nb, B)]
+            for piece in pieces:
+                nc.scalar.activation(out=piece, in_=piece, func=ACT.Sin, scale=TWO_PI)
 
         def weigh(v, half):
             j = v % G
@@ -245,9 +250,7 @@ def tile_ka_attention_heads_mod_pa_kernel(
 
         def add_up(v):
             wave = wave_of.pop(v)
-            bank = pools["sum"].tile([P, WARM], F32)
-            keep_clock(bank[:], 3 if v % G == 0 else 1)
-            total = bank[:, 0 : B * P].rearrange("p (b q) -> p b q", b=B)
+            total = pools["sum"].tile([P, B, P], F32)
             for b in range(B):
                 for t in range(2 * QUAD):
                     half, cl = divmod(t, QUAD)
@@ -271,7 +274,7 @@ def tile_ka_attention_heads_mod_pa_kernel(
             res = pools["results"].tile([P, B, P], F32)
             nc.vector.tensor_tensor(
                 out=res[:],
-                in0=total_of.pop(v),
+                in0=total_of.pop(v)[:],
                 in1=shift_of[o][:, j, :].unsqueeze(1).to_broadcast([P, B, P]),
                 op=ALU.add,
             )
@@ -288,14 +291,8 @@ def tile_ka_attention_heads_mod_pa_kernel(
             b_rows = stage.tile([P, P], BF16)
             g_raw = stage.tile([P, PLANES], BF16)
             ident_bf = stage.tile([P, P], BF16)
-            codes_b = stage.tile([P, ROWS - WARM], U32, align_bytes=64)
-            scales_b = stage.tile([P, ROWS - WARM], U8, align_bytes=64)
-
-            def x_codes(rt):
-                codes, scales, at = codes_a, scales_a, rt * P
-                if at >= WARM:
-                    codes, scales, at = codes_b, scales_b, at - WARM
-                return codes[:, at : at + P].bitcast(FP8X4), scales[:, at : at + P]
+            x_codes = stage.tile([P, ROWS], U32, align_bytes=64)
+            x_scales = stage.tile([P, ROWS], U8, align_bytes=64)
 
             x_rows = x.rearrange("b h p d -> (b h p) d").rearrange(
                 "(b t r) d -> r t b d", r=P, b=B
@@ -317,15 +314,15 @@ def tile_ka_attention_heads_mod_pa_kernel(
                 nc.scalar.copy(out=grouped_w[:, rows, :], in_=mm[:, 0:2, :].rearrange("p u r -> p r u"))
 
             def quantize(rt):
-                codes, scales = x_codes(rt)
+                rows = slice(rt * P, (rt + 1) * P)
                 nc.vector.quantize_mx(
-                    out=codes,
-                    scales=scales,
+                    out=x_codes[:, rows].bitcast(FP8X4),
+                    scales=x_scales[:, rows],
                     in_=grouped[:, rt * 4 * P : (rt + 1) * 4 * P],
                 )
 
             def project(rt, a):
-                codes, scales = x_codes(rt)
+                rows = slice(rt * P, (rt + 1) * P)
                 b, third = divmod(rt, THIRDS)
                 xl_rows = xl[third][:, b, :].rearrange("p (r c) -> p r c", c=COL_BLOCKS)
                 mm = ps_mm.tile([P, 4, P], F32)
@@ -335,8 +332,8 @@ def tile_ka_attention_heads_mod_pa_kernel(
                         out=mm[:, g, :],
                         lhsT=w_words[:, cb * 2 * P : (cb + 1) * 2 * P].bitcast(FP4X4),
                         lhsT_scale=w_scales[:, cb * P : (cb + 1) * P],
-                        rhs=codes,
-                        rhs_scale=scales,
+                        rhs=x_codes[:, rows].bitcast(FP8X4),
+                        rhs_scale=x_scales[:, rows],
                         start=True,
                         stop=True,
                     )
@@ -350,7 +347,7 @@ def tile_ka_attention_heads_mod_pa_kernel(
             def turn(j, third):
                 lo = max(j * QUADS_M, third * QUADS_T)
                 hi = min((j + 1) * QUADS_M, (third + 1) * QUADS_T)
-                for bb in range(B):
+                for bb in range(turned_batches(j)):
                     quads_t = xl[third][:, bb, :].rearrange("p (s c) -> p s c", c=QW)
                     firsts = quads_t[:, lo - third * QUADS_T : hi - third * QUADS_T, 0:TW]
                     mm = ps_mm.tile([P, 4, P], F32)
@@ -361,7 +358,6 @@ def tile_ka_attention_heads_mod_pa_kernel(
             load_x(0)
             nc.vector.memset(w_scales[:].bitcast(I32), 0)
             nc.vector.memset(b_rows[:], 0.0)
-            nc.vector.memset(warm_scales[:].bitcast(I32), 0)
             for quadrant in range(4):
                 nc.sync.dma_start(
                     out=w_scales[32 * quadrant : 32 * quadrant + 4, :].bitcast(I32),
@@ -379,14 +375,6 @@ def tile_ka_attention_heads_mod_pa_kernel(
             for c in range(2 * QUAD):
                 load_coef(c)
             load_shift(0)
-            for quadrant in range(4):
-                nc.sync.dma_start(
-                    out=warm_scales[32 * quadrant : 32 * quadrant + 4, :].bitcast(I32),
-                    in_=lin_w_scales[0, 4 * quadrant : 4 * quadrant + 4, 0:P].bitcast(I32),
-                )
-            nc.sync.dma_start(
-                out=warm_words[:].bitcast(I32), in_=lin_w_words[0][:, 0 : 2 * P].bitcast(I32)
-            )
             for c in range(2 * QUAD, CHUNKS - 2):
                 load_coef(c)
             make_identity(nc, ident_bf[:])
@@ -456,6 +444,7 @@ def tile_ka_attention_heads_mod_pa_kernel(
             negate(2)
             sine_tensor_way(1)
             turn(3, 2)
+            round_off(3)
             sine_vector_way(1)
             turn(4, 2)
 
@@ -475,16 +464,13 @@ def tile_ka_attention_heads_mod_pa_kernel(
         weigh(1, 0)
         add_up(0)
         count_periods(3)
-        round_off(3)
-        scale_up(3)
         negate(3)
-        scale_up(4)
+        scale_up(3)
         round_off(4)
-        scale_up(5)
-        take_off(3)
         turn_coef(2)
-        finish(0)
+        take_off(3)
         weigh(1, 1)
+        finish(0)
         load_shift(1)
         count_periods(4)
         for v in range(2, n_planes):
@@ -493,10 +479,9 @@ def tile_ka_attention_heads_mod_pa_kernel(
             add_up(v - 1)
             if v + 2 < n_planes:
                 negate(v + 2)
+                scale_up(v + 2)
             if v + 3 < n_planes:
                 round_off(v + 3)
-            if v + 4 < n_planes:
-                scale_up(v + 4)
             if v + 1 < n_planes:
                 subtract(v + 1)
             if v + 3 < n_planes:

@@ -41,7 +41,7 @@ FLOPS = 2 * ROWS * D * COLS
 
 
 def turned_batches(j):
-    return B if j % 2 == 0 else B - 1
+    return B - 1 if j == 1 else B
 
 
 def tile_ka_attention_heads_mod_pa_kernel(
@@ -66,12 +66,12 @@ def tile_ka_attention_heads_mod_pa_kernel(
         grouped_w = grouped.bitcast(F32).rearrange("p (r u) -> p r u", u=2)
 
         periods = whole.enter_context(tc.tile_pool(name="periods", bufs=2))
-        scaled = whole.enter_context(tc.tile_pool(name="scaled", bufs=3))
+        scaled = whole.enter_context(tc.tile_pool(name="scaled", bufs=2))
         marks = whole.enter_context(tc.tile_pool(name="marks", bufs=2))
         backs = whole.enter_context(tc.tile_pool(name="backs", bufs=2))
         waves = whole.enter_context(tc.tile_pool(name="waves", bufs=2))
         shifts = whole.enter_context(tc.tile_pool(name="shifts", bufs=2))
-        ps_frac = whole.enter_context(tc.psum_pool(name="ps_frac", bufs=2))
+        ps_frac = whole.enter_context(tc.psum_pool(name="ps_frac", bufs=1))
         ps_coef = whole.enter_context(tc.psum_pool(name="ps_coef", bufs=3))
 
         n_planes = OUT_J * G
@@ -250,7 +250,9 @@ def tile_ka_attention_heads_mod_pa_kernel(
 
         def add_up(v):
             wave = wave_of.pop(v)
-            total = pools["sum"].tile([P, B, P], F32)
+            if v % 2 == 0:
+                total_of[v] = pools["sum"].tile([P, 2, B, P], F32, name="total")
+            total = total_of[v - v % 2][:, v % 2, :, :]
             for b in range(B):
                 for t in range(2 * QUAD):
                     half, cl = divmod(t, QUAD)
@@ -262,24 +264,28 @@ def tile_ka_attention_heads_mod_pa_kernel(
                         stop=(t == 2 * QUAD - 1),
                         is_transpose=True,
                     )
-            total_of[v] = total
 
         def load_shift(o):
-            shift_o = shifts.tile([P, G, P], BF16)
-            nc.sync.dma_start(out=shift_o[:], in_=shift_v[:, o : G * OUT_J : OUT_J, :])
-            shift_of[o] = shift_o
+            shift_o = shifts.tile([P, 2, G, P], BF16)
+            for row in range(2):
+                nc.sync.dma_start(
+                    out=shift_o[:, row, :, :], in_=shift_v[:, o + row : G * OUT_J : OUT_J, :]
+                )
+            shift_of[o // 2] = shift_o[:].rearrange("p r g i -> p (r g) i")
 
         def finish(v):
-            o, j = divmod(v, G)
-            res = pools["results"].tile([P, B, P], F32)
+            rows, at = divmod(v, 2 * G)
+            res = pools["results"].tile([P, 2, B, P], F32)
+            shift_pair = shift_of[rows][:, at : at + 2, :]
             nc.vector.tensor_tensor(
                 out=res[:],
                 in0=total_of.pop(v)[:],
-                in1=shift_of[o][:, j, :].unsqueeze(1).to_broadcast([P, B, P]),
+                in1=shift_pair.unsqueeze(2).to_broadcast([P, 2, B, P]),
                 op=ALU.add,
             )
-            nc.sync.dma_start(out=out_v[:, :, j * OUT_J + o, :], in_=res[:])
-
+            for half in range(2):
+                o, j = divmod(v + half, G)
+                nc.sync.dma_start(out=out_v[:, :, j * OUT_J + o, :], in_=res[:, half, :, :])
 
         whole.enter_context(tc.manual_schedule())
         with ExitStack() as first:
@@ -449,9 +455,9 @@ def tile_ka_attention_heads_mod_pa_kernel(
             turn(4, 2)
 
         pools["waves"] = whole.enter_context(tc.tile_pool(name="late_waves", bufs=1))
-        pools["results"] = whole.enter_context(tc.tile_pool(name="results", bufs=3))
+        pools["results"] = whole.enter_context(tc.tile_pool(name="results", bufs=2))
         pools["coef"] = whole.enter_context(tc.psum_pool(name="ps_late_coef", bufs=1))
-        pools["sum"] = whole.enter_context(tc.psum_pool(name="ps_sum", bufs=1))
+        pools["sum"] = whole.enter_context(tc.psum_pool(name="ps_sum", bufs=2))
         pools["hold"] = whole.enter_context(tc.psum_pool(name="ps_hold", bufs=1))
 
         turn_coef(0, (1,))
@@ -470,11 +476,9 @@ def tile_ka_attention_heads_mod_pa_kernel(
         turn_coef(2)
         take_off(3)
         weigh(1, 1)
-        finish(0)
-        load_shift(1)
         count_periods(4)
         for v in range(2, n_planes):
-            if v % G == 0 and v // G + 1 < OUT_J:
+            if v % (2 * G) == G and v // G + 1 < OUT_J:
                 load_shift(v // G + 1)
             add_up(v - 1)
             if v + 2 < n_planes:
@@ -491,9 +495,10 @@ def tile_ka_attention_heads_mod_pa_kernel(
                 turn_coef(v + 1)
                 sine_vector_way(v + 1)
             weigh(v, 0)
-            finish(v - 1)
             weigh(v, 1)
+            if v % 2 == 0:
+                finish(v - 2)
             if v + 2 < n_planes:
                 take_off(v + 2)
         add_up(n_planes - 1)
-        finish(n_planes - 1)
+        finish(n_planes - 2)

import math
from contextlib import ExitStack

import concourse.mybir as mybir
from concourse.masks import make_identity

F32 = mybir.dt.float32
BF16 = mybir.dt.bfloat16
I32 = mybir.dt.int32
U8 = mybir.dt.uint8
U32 = mybir.dt.uint32
FP8X4 = mybir.dt.float8_e4m3fn_x4
FP4X4 = mybir.dt.float4_e2m1fn_x4
ALU = mybir.AluOpType
ACT = mybir.ActivationFunctionType

P = 128
B, H, POS, D, NF, G = 2, 12, 32, 512, 8, 5
ROWS = B * H * POS
ROWS_B = H * POS
ROW_TILES = ROWS // P
COLS = G * D
COL_BLOCKS = COLS // P
THIRD = P * COL_BLOCKS
CHUNKS = 12
QUAD = 4
QUADS_J = NF * CHUNKS // QUAD
OUT_J = QUADS_J // 2
PLANES = NF * G
WORDS = PLANES // 2
TWO_PI = 2.0 * math.pi
QUADS_M = CHUNKS // QUAD
QW = QUAD * P
QUADS_T = THIRD // QW
TW = P
VW = QW - TW
THIRDS = ROW_TILES // B
OFFSET = 12582912.0

FLOPS = 2 * ROWS * D * COLS


def turned_batches(j):
    return B - 1 if j == 1 else B


def tile_ka_attention_heads_mod_pa_kernel(
    tc, x, lin_w_words, lin_w_scales, lin_b, grid, coef, shift, out
):
    nc = tc.nc
    coef_v = coef.rearrange("(c q i) m j -> q c (i m j)", c=CHUNKS, q=P)
    shift_v = shift.rearrange("o h g p (q i) -> (p q) (o h g) i", i=P)
    out_v = out.rearrange("b h g p (q i) -> (p q) b (h g) i", i=P)

    with ExitStack() as whole:
        keep = whole.enter_context(tc.tile_pool(name="keep", bufs=1))
        ident = keep.tile([P, P], F32)
        make_identity(nc, ident[:])
        xl = [keep.tile([P, B, THIRD], F32, name=f"xl{third}") for third in range(THIRDS)]
        coef_sb = [keep.tile([P, P * PLANES], BF16, name=f"coef{c}") for c in range(CHUNKS)]
        turns = keep.tile([P, PLANES], F32)
        bias_t = keep.tile([P, COL_BLOCKS], F32)

        x_sb = coef_sb[CHUNKS - 1][:, 0 : ROW_TILES * D].rearrange("p (t b d) -> p t b d", b=B, d=D)
        grouped = coef_sb[CHUNKS - 2][:, 0 : ROWS * 4]
        grouped_w = grouped.bitcast(F32).rearrange("p (r u) -> p r u", u=2)

        periods = whole.enter_context(tc.tile_pool(name="periods", bufs=2))
        scaled = whole.enter_context(tc.tile_pool(name="scaled", bufs=2))
        marks = whole.enter_context(tc.tile_pool(name="marks", bufs=2))
        backs = whole.enter_context(tc.tile_pool(name="backs", bufs=2))
        waves = whole.enter_context(tc.tile_pool(name="waves", bufs=2))
        shifts = whole.enter_context(tc.tile_pool(name="shifts", bufs=2))
        ps_frac = whole.enter_context(tc.psum_pool(name="ps_frac", bufs=1))
        ps_coef = whole.enter_context(tc.psum_pool(name="ps_coef", bufs=3))

        n_planes = OUT_J * G
        pools = {}
        coef_banks = []
        k_of, t_of, mark_of, back_of, frac_of, coef_of, wave_of, total_of, shift_of, turned = (
            {}, {}, {}, {}, {}, {}, {}, {}, {}, {},
        )
        held = {}

        def quads(v):
            o, j = divmod(v, G)
            return [divmod(2 * o + half, QUADS_M) for half in range(2)]

        def runs(v):
            j = v % G
            (m0, cq0), (m1, cq1) = quads(v)
            third0, third1 = ((j * QUADS_M + cq) // QUADS_T for cq in (cq0, cq1))
            pieces = [(0, 2, m0, cq0)]
            if m0 != m1 or third0 != third1:
                pieces = [(0, 1, m0, cq0), (1, 1, m1, cq1)]
            found = []
            for first, n, m, cq in pieces:
                third, quad = divmod(j * QUADS_M + cq, QUADS_T)
                x_run = xl[third][:, :, quad * QW : (quad + n) * QW]
                found.append(
                    (
                        first,
                        n,
                        x_run.rearrange("p b (h c) -> p b h c", c=QW),
                        turns[:, j * NF + m : j * NF + m + 1],
                    )
                )
            return found

        def count_periods(v):
            k = periods.tile([P, B, 2, VW], I32)
            for first, n, xq, turn in runs(v):
                nc.gpsimd.tensor_scalar(
                    out=k[:, :, first : first + n, :],
                    in0=xq[:, :, :, TW:QW],
                    scalar1=turn,
                    scalar2=0.0,
                    op0=ALU.mult,
                    op1=ALU.add,
                )
            k_of[v] = k

        def scale_up(v):
            t = scaled.tile([P, B, 2, TW], F32)
            nb = turned_batches(v % G)
            for first, n, xq, turn in runs(v):
                nc.scalar.activation(
                    out=t[:, 0:nb, first : first + n, :],
                    in_=xq[:, 0:nb, :, 0:TW],
                    func=ACT.Copy,
                    scale=turn,
                )
            t_of[v] = t

        def round_off(v):
            mark = marks.tile([P, B, 2, TW], U32)
            for first, n, xq, turn in runs(v):
                nc.scalar.activation(
                    out=mark[:, :, first : first + n, :],
                    in_=xq[:, :, :, 0:TW],
                    func=ACT.Copy,
                    scale=turn,
                    bias=OFFSET,
                )
            mark_of[v] = mark

        def negate(v):
            back = backs.tile([P, B, 2, TW], F32)
            nc.scalar.activation(
                out=back[:], in_=mark_of.pop(v)[:], func=ACT.Copy, scale=-1.0, bias=OFFSET
            )
            back_of[v] = back

        def take_off(v):
            t, back = t_of.pop(v), back_of[v]
            frac = ps_frac.tile([P, B, 2, TW], F32)
            for b in range(turned_batches(v % G)):
                for half in range(2):
                    for step, src in enumerate((t, back)):
                        nc.tensor.matmul(
                            out=frac[:, b, half, :],
                            lhsT=src[:, b, half, :],
                            rhs=ident[:],
                            start=(step == 0),
                            stop=(step == 1),
                            is_transpose=True,
                        )
            frac_of[v] = frac

        def turn_coef(v, halves=(0, 1)):
            j = v % G
            for half in halves:
                m, cq = quads(v)[half]
                key = ((m * G + j) // 2, cq)
                far = cq == 1 and m % 2 == 0 and j == G - 1
                coef_t = held.pop(key) if key in held else turned.pop(key, None)
                if coef_t is None:
                    if far:
                        pool = pools["hold"]
                    else:
                        pool = pools["coef"] if len(coef_banks) % 4 == 3 else ps_coef
                        coef_banks.append(key)
                    coef_t = pool.tile([P, QUAD, P], F32)
                    for cl in range(QUAD):
                        words = coef_sb[cq * QUAD + cl][:].bitcast(F32)
                        nc.tensor.transpose(
                            coef_t[:, cl, :], words[:, key[0] : P * WORDS : WORDS], ident[:]
                        )
                    if far:
                        held[key] = coef_t
                    else:
                        turned[key] = coef_t
                coef_of[v, half] = coef_t

        def subtract(v):
            k = k_of.pop(v)
            pool = pools["waves"] if v % 3 == 2 else waves
            wave = pool.tile([P, B, 2, QW], F32)
            nb = turned_batches(v % G)
            back = back_of.pop(v)
            for first, n, xq, turn in runs(v):
                for b in range(nb, B):
                    nc.vector.scalar_tensor_tensor(
                        out=wave[:, b, first : first + n, 0:TW],
                        in0=xq[:, b, :, 0:TW],
                        scalar=turn,
                        in1=back[:, b, first : first + n, :],
                        op0=ALU.mult,
                        op1=ALU.add,
                    )
            for first, n, xq, turn in reversed(runs(v)):
                for h in reversed(range(n)):
                    nc.vector.scalar_tensor_tensor(
                        out=wave[:, :, first + h, TW:QW],
                        in0=xq[:, :, h, TW:QW],
                        scalar=turn,
                        in1=k[:, :, first + h, :],
                        op0=ALU.mult,
                        op1=ALU.subtract,
                    )
            wave_of[v] = wave

        def sine_tensor_way(v):
            nb = turned_batches(v % G)
            nc.scalar.activation(
                out=wave_of[v][:, 0:nb, :, 0:TW],
                in_=frac_of.pop(v)[:, 0:nb, :, :],
                func=ACT.Sin,
                scale=TWO_PI,
            )

        def sine_vector_way(v):
            nb = turned_batches(v % G)
            pieces = [wave_of[v][:, :, :, TW:QW]]
            pieces += [wave_of[v][:, b, :, 0:TW] for b in range(nb, B)]
            for piece in pieces:
                nc.scalar.activation(out=piece, in_=piece, func=ACT.Sin, scale=TWO_PI)

        def weigh(v, half):
            j = v % G
            m, cq = quads(v)[half]
            pairs = coef_of.pop((v, half))[:].bitcast(BF16).rearrange("p c (q h) -> p c q h", h=2)
            part = wave_of[v][:, :, half, :].rearrange("p b (c q) -> p b c q", c=QUAD)
            nc.vector.tensor_tensor(
                out=part,
                in0=part,
                in1=pairs[:, :, :, (m * G + j) % 2].unsqueeze(1).to_broadcast([P, B, QUAD, P]),
                op=ALU.mult,
            )

        def add_up(v):
            wave = wave_of.pop(v)
            if v % 2 == 0:
                total_of[v] = pools["sum"].tile([P, 2, B, P], F32, name="total")
            total = total_of[v - v % 2][:, v % 2, :, :]
            for b in range(B):
                for t in range(2 * QUAD):
                    half, cl = divmod(t, QUAD)
                    nc.tensor.matmul(
                        out=total[:, b, :],
                        lhsT=wave[:, b, half, cl * P : (cl + 1) * P],
                        rhs=ident[:],
                        start=(t == 0),
                        stop=(t == 2 * QUAD - 1),
                        is_transpose=True,
                    )

        def load_shift(o):
            shift_o = shifts.tile([P, 2, G, P], BF16)
            for row in range(2):
                nc.sync.dma_start(
                    out=shift_o[:, row, :, :], in_=shift_v[:, o + row : G * OUT_J : OUT_J, :]
                )
            shift_of[o // 2] = shift_o[:].rearrange("p r g i -> p (r g) i")

        def finish(v):
            rows, at = divmod(v, 2 * G)
            res = pools["results"].tile([P, 2, B, P], F32)
            shift_pair = shift_of[rows][:, at : at + 2, :]
            nc.vector.tensor_tensor(
                out=res[:],
                in0=total_of.pop(v)[:],
                in1=shift_pair.unsqueeze(2).to_broadcast([P, 2, B, P]),
                op=ALU.add,
            )
            for half in range(2):
                o, j = divmod(v + half, G)
                nc.sync.dma_start(out=out_v[:, :, j * OUT_J + o, :], in_=res[:, half, :, :])

        whole.enter_context(tc.manual_schedule())
        with ExitStack() as first:
            stage = first.enter_context(tc.tile_pool(name="stage", bufs=1))
            ps_mm = first.enter_context(tc.psum_pool(name="ps_mm", bufs=3))

            w_words = stage.tile([P, 2 * COLS], U8, align_bytes=64)
            w_scales = stage.tile([P, COLS], U8, align_bytes=64)
            b_rows = stage.tile([P, P], BF16)
            g_raw = stage.tile([P, PLANES], BF16)
            ident_bf = stage.tile([P, P], BF16)
            x_codes = stage.tile([P, ROWS], U32, align_bytes=64)
            x_scales = stage.tile([P, ROWS], U8, align_bytes=64)

            x_rows = x.rearrange("b h p d -> (b h p) d").rearrange(
                "(b t r) d -> r t b d", r=P, b=B
            )

            def load_x(third):
                nc.sync.dma_start(out=x_sb[:, third, :, :], in_=x_rows[:, third, :, :])

            def load_coef(c):
                nc.sync.dma_start(out=coef_sb[c][:], in_=coef_v[:, c, :])

            def group_x(rt):
                rows = slice(rt * P, (rt + 1) * P)
                b, third = divmod(rt, THIRDS)
                mm = ps_mm.tile([P, 4, P], F32)
                x_words = x_sb[:, third, b, :].bitcast(F32)
                for u in range(2):
                    nc.tensor.transpose(mm[:, u, :], x_words[:, u : D // 2 : 2], ident[:])
                nc.scalar.copy(out=grouped_w[:, rows, :], in_=mm[:, 0:2, :].rearrange("p u r -> p r u"))

            def quantize(rt):
                rows = slice(rt * P, (rt + 1) * P)
                nc.vector.quantize_mx(
                    out=x_codes[:, rows].bitcast(FP8X4),
                    scales=x_scales[:, rows],
                    in_=grouped[:, rt * 4 * P : (rt + 1) * 4 * P],
                )

            def project(rt, a):
                rows = slice(rt * P, (rt + 1) * P)
                b, third = divmod(rt, THIRDS)
                xl_rows = xl[third][:, b, :].rearrange("p (r c) -> p r c", c=COL_BLOCKS)
                mm = ps_mm.tile([P, 4, P], F32)
                for g in range(4):
                    cb = 4 * a + g
                    nc.tensor.matmul_mx(
                        out=mm[:, g, :],
                        lhsT=w_words[:, cb * 2 * P : (cb + 1) * 2 * P].bitcast(FP4X4),
                        lhsT_scale=w_scales[:, cb * P : (cb + 1) * P],
                        rhs=x_codes[:, rows].bitcast(FP8X4),
                        rhs_scale=x_scales[:, rows],
                        start=True,
                        stop=True,
                    )
                nc.vector.tensor_tensor(
                    out=xl_rows[:, :, 4 * a : 4 * a + 4],
                    in0=mm[:].rearrange("p g r -> p r g"),
                    in1=bias_t[:, 4 * a : 4 * a + 4].unsqueeze(1).to_broadcast([P, P, 4]),
                    op=ALU.add,
                )

            def turn(j, third):
                lo = max(j * QUADS_M, third * QUADS_T)
                hi = min((j + 1) * QUADS_M, (third + 1) * QUADS_T)
                for bb in range(turned_batches(j)):
                    quads_t = xl[third][:, bb, :].rearrange("p (s c) -> p s c", c=QW)
                    firsts = quads_t[:, lo - third * QUADS_T : hi - third * QUADS_T, 0:TW]
                    mm = ps_mm.tile([P, 4, P], F32)
                    for s in range(hi - lo):
                        nc.tensor.transpose(mm[:, s, :], firsts[:, s, :], ident[:])
                    nc.scalar.copy(out=firsts, in_=mm[:, 0 : hi - lo, :])

            load_x(0)
            nc.vector.memset(w_scales[:].bitcast(I32), 0)
            nc.vector.memset(b_rows[:], 0.0)
            for quadrant in range(4):
                nc.sync.dma_start(
                    out=w_scales[32 * quadrant : 32 * quadrant + 4, :].bitcast(I32),
                    in_=lin_w_scales[0, 4 * quadrant : 4 * quadrant + 4, :].bitcast(I32),
                )
            nc.sync.dma_start(out=w_words[:].bitcast(I32), in_=lin_w_words[0].bitcast(I32))
            nc.sync.dma_start(
                out=b_rows[0:COL_BLOCKS, :], in_=lin_b.rearrange("(c i) -> c i", i=P)
            )
            nc.sync.dma_start(
                out=g_raw[:], in_=grid.rearrange("j m -> (j m)").partition_broadcast(P)
            )
            load_x(1)
            load_x(2)
            for c in range(2 * QUAD):
                load_coef(c)
            load_shift(0)
            for c in range(2 * QUAD, CHUNKS - 2):
                load_coef(c)
            make_identity(nc, ident_bf[:])

            blocks = range(COL_BLOCKS // 4)
            for rt in (0, THIRDS):
                group_x(rt)
                quantize(rt)
            nc.vector.tensor_scalar(
                out=turns[:], in0=g_raw[:], scalar1=1.0 / TWO_PI, scalar2=None, op0=ALU.mult
            )
            mm = ps_mm.tile([P, 8, P], BF16)
            nc.tensor.transpose(mm[:, 0, :], b_rows[:], ident_bf[:])
            nc.vector.tensor_copy(out=bias_t[:], in_=mm[:, 0, 0:COL_BLOCKS])
            for a in blocks:
                project(0, a)
            for rt in (1, THIRDS + 1):
                group_x(rt)
                quantize(rt)
            for a in blocks:
                project(THIRDS, a)
            for a in blocks[:2]:
                project(1, a)
            turn(0, 0)
            turn(1, 0)
            count_periods(0)
            count_periods(1)
            scale_up(0)
            round_off(0)
            for a in blocks[2:]:
                project(1, a)
            for rt in (2, THIRDS + 2):
                group_x(rt)
                quantize(rt)
            for c in range(CHUNKS - 2, CHUNKS):
                load_coef(c)
            negate(0)
            for a in blocks[:2]:
                project(THIRDS + 1, a)
            take_off(0)
            for a in blocks[2:]:
                project(THIRDS + 1, a)
            subtract(0)
            sine_tensor_way(0)
            sine_vector_way(0)
            for a in blocks[:2]:
                project(2, a)
            turn(1, 1)
            scale_up(1)
            round_off(1)
            turn_coef(0, (0,))
            for a in blocks[2:]:
                project(2, a)
            turn(2, 1)
            turn(3, 1)
            negate(1)
            scale_up(2)
            round_off(2)
            weigh(0, 0)
            count_periods(2)
            for a in blocks[:3]:
                project(THIRDS + 2, a)
            take_off(1)
            for a in blocks[3:]:
                project(THIRDS + 2, a)
            subtract(1)
            negate(2)
            sine_tensor_way(1)
            turn(3, 2)
            round_off(3)
            sine_vector_way(1)
            turn(4, 2)

        pools["waves"] = whole.enter_context(tc.tile_pool(name="late_waves", bufs=1))
        pools["results"] = whole.enter_context(tc.tile_pool(name="results", bufs=2))
        pools["coef"] = whole.enter_context(tc.psum_pool(name="ps_late_coef", bufs=1))
        pools["sum"] = whole.enter_context(tc.psum_pool(name="ps_sum", bufs=2))
        pools["hold"] = whole.enter_context(tc.psum_pool(name="ps_hold", bufs=1))

        turn_coef(0, (1,))
        take_off(2)
        weigh(0, 1)
        subtract(2)
        sine_tensor_way(2)
        sine_vector_way(2)
        turn_coef(1)
        weigh(1, 0)
        add_up(0)
        count_periods(3)
        negate(3)
        scale_up(3)
        round_off(4)
        turn_coef(2)
        take_off(3)
        weigh(1, 1)
        count_periods(4)
        for v in range(2, n_planes):
            if v % (2 * G) == G and v // G + 1 < OUT_J:
                load_shift(v // G + 1)
            add_up(v - 1)
            if v + 2 < n_planes:
                negate(v + 2)
                scale_up(v + 2)
            if v + 3 < n_planes:
                round_off(v + 3)
            if v + 1 < n_planes:
                subtract(v + 1)
            if v + 3 < n_planes:
                count_periods(v + 3)
            if v + 1 < n_planes:
                sine_tensor_way(v + 1)
                turn_coef(v + 1)
                sine_vector_way(v + 1)
            weigh(v, 0)
            weigh(v, 1)
            if v % 2 == 0:
                finish(v - 2)
            if v + 2 < n_planes:
                take_off(v + 2)
        add_up(n_planes - 1)
        finish(n_planes - 2)
